import numpy as np
import ml_dtypes


def mxq(x, axis, fmt="e4m3"):
    dtype, down = {"e4m3": (ml_dtypes.float8_e4m3fn, 7), "e5m2": (ml_dtypes.float8_e5m2, 14)}[fmt]
    v = np.moveaxis(np.asarray(x, np.float32).astype(ml_dtypes.bfloat16).astype(np.float64), axis, -1)
    blocks = v.reshape(v.shape[:-1] + (-1, 32))
    amax = np.abs(blocks).max(-1, keepdims=True)
    byte = np.maximum(np.where(amax > 0, np.frexp(amax)[1] - 1 + 127, 0) - down, 1)
    scale = np.exp2(byte - 127.0)
    codes = (blocks / scale).astype(np.float32).astype(dtype).astype(np.float64)
    return np.moveaxis((codes * scale).reshape(v.shape), -1, axis)


WIDE = False


def mx_kscale(k):
    if not WIDE:
        return np.ones(k)
    levels = np.array([30, -30])
    if k % 512:
        return np.exp2(np.random.permutation(np.resize(levels, k // 32))).repeat(32)
    a = np.empty((k // 512, 16))
    for p in range(k // 512):
        a[p, :8] = np.random.permutation(np.resize(levels, 8))
        for g in range(8):
            far = levels[np.abs(levels - a[p, g]) >= 10]
            a[p, g + 8] = far[np.random.randint(len(far))]
    return np.exp2(a.ravel()).repeat(32)


BF16 = ml_dtypes.bfloat16


def bf(x):
    return np.asarray(x, np.float32).astype(BF16)


def f64(x):
    return np.asarray(x).astype(np.float64)


B, S, M, H, HKV, DH, R_T, R_H, R_W = 1, 1024, 1536, 12, 2, 128, 16, 24, 24
SECT = (2 * R_T, 2 * R_H, 2 * R_W)
NC = len(SECT)


def rotate_half(x):
    h = x.shape[-1] // 2
    return np.concatenate((-x[..., h:], x[..., :h]), axis=-1)


def mrope_combine(t):
    parts, off = [], 0
    for i, sz in enumerate(SECT):
        parts.append(t[i % NC, :, :, off:off + sz])
        off += sz
    return np.concatenate(parts, axis=-1)


def setup_inputs():
    s = mx_kscale(M)
    sd = 1.0 / np.sqrt(M)
    return {"hidden_states": bf(np.random.standard_normal((B, S, M)) * s),
            "cos": bf(np.random.standard_normal((NC, B, S, DH))),
            "sin": bf(np.random.standard_normal((NC, B, S, DH))),
            "Wq": bf(np.random.standard_normal((M, H, DH)) * sd / s[:, None, None]),
            "bq": bf(np.random.standard_normal((H, DH)) * 0.3),
            "Wk": bf(np.random.standard_normal((M, HKV, DH)) * sd / s[:, None, None]),
            "bk": bf(np.random.standard_normal((HKV, DH)) * 0.3),
            "Wv": bf(np.random.standard_normal((M, HKV, DH)) * sd / s[:, None, None]),
            "bv": bf(np.random.standard_normal((HKV, DH)) * 0.3)}


def reference(hidden_states, cos, sin, Wq, bq, Wk, bk, Wv, bv):
    xq = mxq(f64(hidden_states), 2, "e5m2")
    q = (xq @ mxq(f64(Wq).reshape(M, H * DH), 0, "e4m3")).reshape(B, S, H, DH) + f64(bq)
    k = (xq @ mxq(f64(Wk).reshape(M, HKV * DH), 0, "e4m3")).reshape(B, S, HKV, DH) + f64(bk)
    v = (xq @ mxq(f64(Wv).reshape(M, HKV * DH), 0, "e4m3")).reshape(B, S, HKV, DH) + f64(bv)
    cos_c = mrope_combine(f64(cos))[:, :, None, :]
    sin_c = mrope_combine(f64(sin))[:, :, None, :]
    q_rot = q * cos_c + rotate_half(q) * sin_c
    k_rot = k * cos_c + rotate_half(k) * sin_c
    return q_rot, k_rot, v

@@ -1,0 +1,339 @@
+from contextlib import ExitStack
+
+import concourse.mybir as mybir
+from concourse.masks import make_identity
+
+S, M, DH = 1024, 1536, 128
+Q_HEADS, KV_HEADS = 12, 2
+FLOPS = 2 * S * M * (Q_HEADS + 2 * KV_HEADS) * DH
+BYTES = 2 * (S * M + (M + 1) * (Q_HEADS + 2 * KV_HEADS) * DH + 2 * S * DH) + 4 * S * (Q_HEADS + 2 * KV_HEADS) * DH
+
+F32 = mybir.dt.float32
+BF16 = mybir.dt.bfloat16
+U32 = mybir.dt.uint32
+U8 = mybir.dt.uint8
+E4M3X4 = mybir.dt.float8_e4m3fn_x4
+E5M2X4 = mybir.dt.float8_e5m2_x4
+ADD = mybir.AluOpType.add
+MULT = mybir.AluOpType.mult
+IDENTITY = mybir.ActivationFunctionType.Identity
+
+P = 128
+PACK = 4
+PASSES = M // (P * PACK)
+HALF_D = DH // 2
+TILES = 4
+HALF_TOK = TILES * P
+PAIR_W = 2 * DH
+ROPE_PAIRS = (Q_HEADS + KV_HEADS) // 2
+V_PAIR = ROPE_PAIRS
+SECTIONS = ((0, 32), (32, 80), (80, 128))
+BV_ROW = Q_HEADS + KV_HEADS
+
+
+def tile_qwen2vlattention_pa_kernel(tc, hidden_states, cos, sin, Wq, bq, Wk, bk, Wv, bv, out_0, out_1, out_2):
+    nc = tc.nc
+
+    with ExitStack() as ctx:
+        keep = ctx.enter_context(tc.tile_pool(name="keep", bufs=1))
+        work = ctx.enter_context(tc.tile_pool(name="work", bufs=3))
+        psum = ctx.enter_context(tc.psum_pool(name="psum", bufs=2))
+        ctx.enter_context(tc.manual_schedule())
+
+        x_hbm = hidden_states[0].rearrange("(t p) m -> p t m", p=P)
+        x_raw = {}
+        w_raw = {}
+        cos_tok = {}
+        sin_tok = {}
+
+        def load_x(duo):
+            x_raw[duo] = keep.tile([P, 2, M], BF16, name="x_raw%d" % duo)
+            nc.sync.dma_start(out=x_raw[duo][:], in_=x_hbm[:, 2 * duo : 2 * duo + 2, :])
+
+        def load_w(w_hbm, first_pair, pairs, col0):
+            rows = w_hbm.rearrange("(c p j) h d -> c p j (h d)", p=P, j=PACK)
+            for c in range(PASSES):
+                raw = keep.tile([P, PACK, pairs * PAIR_W], BF16, name="w_raw%d_%d" % (first_pair, c))
+                nc.sync.dma_start(out=raw[:], in_=rows[c][:, :, col0 : col0 + pairs * PAIR_W])
+                for s in range(pairs):
+                    w_raw[first_pair + s, c] = raw[:, :, s * PAIR_W : (s + 1) * PAIR_W]
+
+        def load_tables(half):
+            for table, tok, label in ((cos, cos_tok, "cos"), (sin, sin_tok, "sin")):
+                tok[half] = keep.tile([P, TILES, DH], BF16, name="%s_tok%d" % (label, half))
+                for comp, (d0, d1) in enumerate(SECTIONS):
+                    rows = table[comp][0].rearrange("(t p) d -> p t d", p=P)
+                    nc.sync.dma_start(out=tok[half][:, :, d0:d1], in_=rows[:, TILES * half : TILES * (half + 1), d0:d1])
+
+        load_x(0)
+        load_x(1)
+        load_w(Wk, 0, 1, 0)
+        load_tables(0)
+        load_x(2)
+        load_x(3)
+        load_w(Wq, 1, 2, 0)
+        load_tables(1)
+        load_w(Wq, 3, 2, 2 * PAIR_W)
+        load_w(Wq, 5, 2, 4 * PAIR_W)
+        load_w(Wv, V_PAIR, 1, 0)
+
+        bias_rows = keep.tile([P, PAIR_W], BF16)
+        nc.vector.memset(bias_rows[:], 0.0)
+        nc.scalar.dma_start(out=bias_rows[0:KV_HEADS, 0:DH], in_=bk)
+        nc.scalar.dma_start(out=bias_rows[KV_HEADS:BV_ROW, 0:DH], in_=bq)
+        nc.scalar.dma_start(out=bias_rows[BV_ROW : BV_ROW + 1, :], in_=bv.rearrange("(o h) d -> o (h d)", o=1))
+
+        ident = keep.tile([P, P], F32)
+        make_identity(nc, ident[:])
+        swap = keep.tile([P, P], F32)
+        nc.gpsimd.tensor_copy(out=swap[:, 0:HALF_D], in_=ident[:, HALF_D:P])
+        nc.gpsimd.tensor_copy(out=swap[:, HALF_D:P], in_=ident[:, 0:HALF_D])
+        ident_bf = keep.tile([P, P], BF16)
+        make_identity(nc, ident_bf[:])
+
+        x_codes = {}
+        x_scales = {}
+        for half in range(2):
+            for c in range(PASSES):
+                x_codes[half, c] = keep.tile([P, HALF_TOK], U32, name="x_codes%d_%d" % (half, c), align_bytes=64)
+                x_scales[half, c] = keep.tile([P, HALF_TOK], U8, name="x_scales%d_%d" % (half, c), align_bytes=64)
+        x_bank = {}
+        x_grouped = {}
+        w_grouped = {}
+        w_codes = {}
+        w_scales = {}
+        sums = {}
+        cos_part = {}
+        sin_part = {}
+        biased = {}
+        turned = {}
+        result = {}
+
+        def copy_on(engine, out, in_):
+            if engine == "scalar":
+                nc.scalar.copy(out=out, in_=in_)
+            else:
+                nc.vector.tensor_copy(out=out, in_=in_)
+
+        def transpose_x(duo, c, tag):
+            x_bank[duo, c] = psum.tile([P, 2, 2, P], F32, name="x_bank", tag=tag)
+            words = x_raw[duo][:].bitcast(F32)
+            for j in range(2):
+                for u in range(2):
+                    nc.tensor.transpose(x_bank[duo, c][:, j, u, :], words[:, j, 256 * c + u : 256 * (c + 1) : 2], ident[:])
+
+        def group_x(duo, c, engine):
+            x_grouped[duo, c] = work.tile([P, 2 * P * PACK], BF16, name="x_grouped", bufs=6, align_bytes=64)
+            copy_on(
+                engine,
+                x_grouped[duo, c][:].bitcast(F32).rearrange("p (j r u) -> p j r u", j=2, u=2),
+                x_bank[duo, c][:].rearrange("p j u r -> p j r u"),
+            )
+
+        def quantize_x(duo, c):
+            half, cols = duo // 2, slice((duo % 2) * 2 * P, (duo % 2 + 1) * 2 * P)
+            nc.vector.quantize_mx(
+                out=x_codes[half, c][:, cols].bitcast(E5M2X4), scales=x_scales[half, c][:, cols], in_=x_grouped[duo, c][:]
+            )
+
+        def group_w(pair, c, engine):
+            w_grouped[pair, c] = work.tile([P, PAIR_W * PACK], BF16, name="w_grouped", bufs=5, align_bytes=64)
+            copy_on(
+                engine,
+                w_grouped[pair, c][:].rearrange("p (n i t) -> p n t i", i=4, t=PACK),
+                w_raw[pair, c].rearrange("p t (n i) -> p n t i", i=4),
+            )
+
+        def quantize_w(pair, c):
+            w_codes[pair, c] = keep.tile([P, PAIR_W], U32, name="w_codes%d_%d" % (pair, c), align_bytes=64)
+            w_scales[pair, c] = keep.tile([P, PAIR_W], U8, name="w_scales%d_%d" % (pair, c), align_bytes=64)
+            nc.vector.quantize_mx(out=w_codes[pair, c][:].bitcast(E4M3X4), scales=w_scales[pair, c][:], in_=w_grouped[pair, c][:])
+
+        def project(pair, half):
+            for h in range(2):
+                sums[pair, half, h] = psum.tile([P, HALF_TOK], F32, name="sums", tag="mx%d" % half)
+                cols = slice(h * DH, (h + 1) * DH)
+                for c in range(PASSES):
+                    nc.tensor.matmul_mx(
+                        out=sums[pair, half, h][:],
+                        lhsT=w_codes[pair, c][:, cols].bitcast(E4M3X4),
+                        lhsT_scale=w_scales[pair, c][:, cols],
+                        rhs=x_codes[half, c][:].bitcast(E5M2X4),
+                        rhs_scale=x_scales[half, c][:],
+                        start=(c == 0),
+                        stop=(c == PASSES - 1),
+                    )
+
+        def bias_col(pair, h):
+            col = PAIR_W + 2 * pair + h
+            return bias_sb[:, col : col + 1]
+
+        def store(pair, tiles, src):
+            if pair == 0:
+                dst, col0 = out_1, 0
+            elif pair == V_PAIR:
+                dst, col0 = out_2, 0
+            else:
+                dst, col0 = out_0, (pair - 1) * PAIR_W
+            rows = dst[0].rearrange("(t p) h d -> p t (h d)", p=P)
+            nc.sync.dma_start(out=rows[:, tiles, col0 : col0 + PAIR_W], in_=src)
+
+        def multiply_chan(pair):
+            for h in range(2):
+                cos_part[pair, 0, h] = work.tile([P, HALF_TOK], F32, name="cos_chan")
+                sin_part[pair, 0, h] = work.tile([P, HALF_TOK], F32, name="sin_chan")
+                for part, k in ((cos_part, 0), (sin_part, 1)):
+                    nc.vector.scalar_tensor_tensor(
+                        out=part[pair, 0, h][:], in0=sums[pair, 0, h][:], scalar=bias_col(pair, h), in1=tables_chan[:, k, :], op0=ADD, op1=MULT
+                    )
+
+        def turn_and_add(pair):
+            for h in range(2):
+                turned[pair, 0, h] = psum.tile([P, TILES, DH], F32, name="turned", tag="tr0")
+                for t in range(TILES):
+                    toks = slice(t * P, (t + 1) * P)
+                    nc.tensor.matmul(turned[pair, 0, h][:, t, :], lhsT=cos_part[pair, 0, h][:, toks], rhs=ident[:], is_transpose=True, start=True, stop=False)
+                    nc.tensor.matmul(turned[pair, 0, h][:, t, :], lhsT=sin_part[pair, 0, h][:, toks], rhs=swap[:], is_transpose=True, start=False, stop=True)
+
+        def finish_chan(pair):
+            result[pair, 0] = work.tile([P, TILES, PAIR_W], F32, name="result0")
+            for h in range(2):
+                nc.scalar.copy(out=result[pair, 0][:, :, h * DH : (h + 1) * DH], in_=turned[pair, 0, h][:])
+            store(pair, slice(0, TILES), result[pair, 0][:])
+
+        def add_bias(pair):
+            for h in range(2):
+                biased[pair, h] = work.tile([P, HALF_TOK], F32, name="biased", bufs=4)
+                nc.scalar.activation(out=biased[pair, h][:], in_=sums[pair, 1, h][:], func=IDENTITY, bias=bias_col(pair, h))
+
+        def turn(pair):
+            for h in range(2):
+                turned[pair, 1, h] = psum.tile([P, TILES, DH], F32, name="turned", tag="tr1")
+                for t in range(TILES):
+                    nc.tensor.transpose(turned[pair, 1, h][:, t, :], biased[pair, h][:, t * P : (t + 1) * P], ident[:])
+
+        def rotate_tok(pair):
+            result[pair, 1] = work.tile([P, TILES, PAIR_W], F32, name="result1")
+            for h in range(2):
+                u = turned[pair, 1, h]
+                cos_part[pair, 1, h] = work.tile([P, TILES, DH], F32, name="cos_tokp")
+                sin_part[pair, 1, h] = work.tile([P, TILES, DH], F32, name="sin_tokp")
+                nc.vector.tensor_tensor(out=cos_part[pair, 1, h][:], in0=u[:], in1=cos_tok[1][:], op=MULT)
+                nc.vector.tensor_tensor(out=sin_part[pair, 1, h][:, :, 0:HALF_D], in0=u[:, :, HALF_D:DH], in1=sin_tok[1][:, :, 0:HALF_D], op=MULT)
+                nc.vector.tensor_tensor(out=sin_part[pair, 1, h][:, :, HALF_D:DH], in0=u[:, :, 0:HALF_D], in1=sin_tok[1][:, :, HALF_D:DH], op=MULT)
+                nc.gpsimd.tensor_tensor(out=result[pair, 1][:, :, h * DH : (h + 1) * DH], in0=cos_part[pair, 1, h][:], in1=sin_part[pair, 1, h][:], op=ADD)
+            store(pair, slice(TILES, 2 * TILES), result[pair, 1][:])
+
+        def project_v(duo):
+            half = duo // 2
+            sums[V_PAIR, duo] = psum.tile([P, 2, PAIR_W], F32, name="sums_v", tag="mx%d" % half)
+            for j in range(2):
+                t = (duo % 2) * 2 + j
+                toks = slice(t * P, (t + 1) * P)
+                for c in range(PASSES):
+                    nc.tensor.matmul_mx(
+                        out=sums[V_PAIR, duo][:, j, :],
+                        lhsT=x_codes[half, c][:, toks].bitcast(E5M2X4),
+                        lhsT_scale=x_scales[half, c][:, toks],
+                        rhs=w_codes[V_PAIR, c][:].bitcast(E4M3X4),
+                        rhs_scale=w_scales[V_PAIR, c][:],
+                        start=(c == 0),
+                        stop=(c == PASSES - 1),
+                    )
+
+        def finish_v(duo):
+            res = work.tile([P, 2, PAIR_W], F32, name="result_v", bufs=4)
+            nc.vector.tensor_tensor(
+                out=res[:], in0=sums[V_PAIR, duo][:], in1=bias_sb[:, 0:PAIR_W].unsqueeze(1).to_broadcast([P, 2, PAIR_W]), op=ADD
+            )
+            store(V_PAIR, slice(2 * duo, 2 * duo + 2), res[:])
+
+        for c, tag in enumerate(("mx1", "tr0", "tr1")):
+            transpose_x(0, c, tag)
+        group_x(0, 0, "vector")
+        group_x(0, 1, "scalar")
+        group_x(0, 2, "vector")
+        for c, tag in enumerate(("mx1", "tr0", "tr1")):
+            transpose_x(1, c, tag)
+            group_x(1, c, "scalar")
+        for c in range(PASSES):
+            quantize_x(0, c)
+        group_w(0, 0, "vector")
+        group_w(0, 1, "vector")
+        quantize_w(0, 0)
+        quantize_x(1, 0)
+        group_w(0, 2, "vector")
+        quantize_w(0, 1)
+        quantize_x(1, 1)
+        quantize_w(0, 2)
+        quantize_x(1, 2)
+
+        bias_bank = psum.tile([P, PAIR_W + BV_ROW], F32, tag="mx1")
+        nc.tensor.matmul(bias_bank[:, 0:PAIR_W], lhsT=ident_bf[:, BV_ROW : BV_ROW + 1].to_broadcast([P, P]), rhs=bias_rows[:], start=True, stop=True)
+        nc.tensor.matmul(bias_bank[:, PAIR_W : PAIR_W + BV_ROW], lhsT=bias_rows[:, 0:DH], rhs=ident_bf[:, 0:BV_ROW], start=True, stop=True)
+        bias_sb = keep.tile([P, PAIR_W + BV_ROW], F32)
+        nc.scalar.activation(out=bias_sb[:], in_=bias_bank[:], func=IDENTITY)
+
+        project(0, 0)
+
+        sin_swapped = keep.tile([P, TILES, DH], BF16)
+        nc.vector.tensor_copy(out=sin_swapped[:, :, 0:HALF_D], in_=sin_tok[0][:, :, HALF_D:DH])
+        nc.vector.tensor_scalar(out=sin_swapped[:, :, HALF_D:DH], in0=sin_tok[0][:, :, 0:HALF_D], scalar1=-1.0, scalar2=None, op0=MULT)
+        table_bank = psum.tile([P, 2, TILES, P], BF16, tag="tr0")
+        for k, table in enumerate((cos_tok[0], sin_swapped)):
+            for t in range(TILES):
+                nc.tensor.transpose(table_bank[:, k, t, :], table[:, t, :], ident_bf[:])
+        tables_chan = keep.tile([P, 2, HALF_TOK], BF16)
+        nc.scalar.copy(out=tables_chan[:], in_=table_bank[:].rearrange("p k t r -> p k (t r)"))
+
+        multiply_chan(0)
+        for duo in (2, 3):
+            for c, tag in enumerate(("tr1", "mx1", "tr0")):
+                transpose_x(duo, c, tag)
+                group_x(duo, c, "scalar")
+        for c in range(PASSES):
+            quantize_x(2, c)
+        group_w(1, 0, "vector")
+        for c in range(PASSES):
+            quantize_x(3, c)
+        turn_and_add(0)
+        project(0, 1)
+        group_w(1, 1, "scalar")
+        quantize_w(1, 0)
+        group_w(1, 2, "vector")
+        quantize_w(1, 1)
+        nc.vector.tensor_scalar(out=sin_tok[1][:, :, 0:HALF_D], in0=sin_tok[1][:, :, 0:HALF_D], scalar1=-1.0, scalar2=None, op0=MULT)
+        quantize_w(1, 2)
+        group_w(2, 0, "vector")
+        group_w(2, 1, "scalar")
+        add_bias(0)
+
+        last = ROPE_PAIRS - 1
+        for pair in range(1, ROPE_PAIRS):
+            project(pair, 0)
+            finish_chan(pair - 1)
+            multiply_chan(pair)
+            project(pair, 1)
+            group_w(pair + 1, 2, "scalar")
+            for c in range(PASSES):
+                quantize_w(pair + 1, c)
+            add_bias(pair)
+            turn(pair - 1)
+            rotate_tok(pair - 1)
+            if pair < last:
+                turn_and_add(pair)
+                group_w(pair + 2, 0, "scalar")
+                group_w(pair + 2, 1, "scalar")
+
+        project_v(0)
+        project_v(1)
+        turn_and_add(last)
+        finish_v(0)
+        finish_v(1)
+        finish_chan(last)
+        turn(last)
+        project_v(2)
+        project_v(3)
+        rotate_tok(last)
+        finish_v(2)
+        finish_v(3)

@@ -28,7 +28,8 @@ PAIR_W = 2 * DH
 ROPE_PAIRS = (Q_HEADS + KV_HEADS) // 2
 V_PAIR = ROPE_PAIRS
 SECTIONS = ((0, 32), (32, 80), (80, 128))
-BV_ROW = Q_HEADS + KV_HEADS
+HEADS = Q_HEADS + 2 * KV_HEADS
+SCALAR_COLS = 192
 
 
 def tile_qwen2vlattention_pa_kernel(tc, hidden_states, cos, sin, Wq, bq, Wk, bk, Wv, bv, out_0, out_1, out_2):
@@ -58,38 +59,38 @@ def tile_qwen2vlattention_pa_kernel(tc, hidden_states, cos, sin, Wq, bq, Wk, bk,
                 for s in range(pairs):
                     w_raw[first_pair + s, c] = raw[:, :, s * PAIR_W : (s + 1) * PAIR_W]
 
-        def load_tables(half):
-            for table, tok, label in ((cos, cos_tok, "cos"), (sin, sin_tok, "sin")):
-                tok[half] = keep.tile([P, TILES, DH], BF16, name="%s_tok%d" % (label, half))
-                for comp, (d0, d1) in enumerate(SECTIONS):
-                    rows = table[comp][0].rearrange("(t p) d -> p t d", p=P)
-                    nc.sync.dma_start(out=tok[half][:, :, d0:d1], in_=rows[:, TILES * half : TILES * (half + 1), d0:d1])
+        def load_table(table, tok, label, half):
+            tok[half] = keep.tile([P, TILES, DH], BF16, name="%s_tok%d" % (label, half))
+            for comp, (d0, d1) in enumerate(SECTIONS):
+                rows = table[comp][0].rearrange("(t p) d -> p t d", p=P)
+                nc.sync.dma_start(out=tok[half][:, :, d0:d1], in_=rows[:, TILES * half : TILES * (half + 1), d0:d1])
 
-        load_x(0)
-        load_x(1)
+        for duo in range(4):
+            load_x(duo)
         load_w(Wk, 0, 1, 0)
-        load_tables(0)
-        load_x(2)
-        load_x(3)
-        load_w(Wq, 1, 2, 0)
-        load_tables(1)
+        load_table(sin, sin_tok, "sin", 0)
+        load_w(Wq, 1, 1, 0)
+        load_table(cos, cos_tok, "cos", 0)
+        load_w(Wq, 2, 1, PAIR_W)
+        load_table(cos, cos_tok, "cos", 1)
+        load_table(sin, sin_tok, "sin", 1)
         load_w(Wq, 3, 2, 2 * PAIR_W)
         load_w(Wq, 5, 2, 4 * PAIR_W)
         load_w(Wv, V_PAIR, 1, 0)
 
-        bias_rows = keep.tile([P, PAIR_W], BF16)
+        bias_rows = keep.tile([P, DH], BF16)
         nc.vector.memset(bias_rows[:], 0.0)
-        nc.scalar.dma_start(out=bias_rows[0:KV_HEADS, 0:DH], in_=bk)
-        nc.scalar.dma_start(out=bias_rows[KV_HEADS:BV_ROW, 0:DH], in_=bq)
-        nc.scalar.dma_start(out=bias_rows[BV_ROW : BV_ROW + 1, :], in_=bv.rearrange("(o h) d -> o (h d)", o=1))
+        nc.scalar.dma_start(out=bias_rows[0:KV_HEADS, :], in_=bk)
+        nc.scalar.dma_start(out=bias_rows[KV_HEADS : KV_HEADS + Q_HEADS, :], in_=bq)
+        nc.scalar.dma_start(out=bias_rows[KV_HEADS + Q_HEADS : HEADS, :], in_=bv)
 
         ident = keep.tile([P, P], F32)
         make_identity(nc, ident[:])
+        ident_bf = keep.tile([P, P], BF16)
+        make_identity(nc, ident_bf[:])
         swap = keep.tile([P, P], F32)
         nc.gpsimd.tensor_copy(out=swap[:, 0:HALF_D], in_=ident[:, HALF_D:P])
         nc.gpsimd.tensor_copy(out=swap[:, HALF_D:P], in_=ident[:, 0:HALF_D])
-        ident_bf = keep.tile([P, P], BF16)
-        make_identity(nc, ident_bf[:])
 
         x_codes = {}
         x_scales = {}
@@ -107,7 +108,8 @@ def tile_qwen2vlattention_pa_kernel(tc, hidden_states, cos, sin, Wq, bq, Wk, bk,
         sin_part = {}
         biased = {}
         turned = {}
-        result = {}
+        tables_chan = {}
+        results = {}
 
         def copy_on(engine, out, in_):
             if engine == "scalar":
@@ -123,7 +125,7 @@ def tile_qwen2vlattention_pa_kernel(tc, hidden_states, cos, sin, Wq, bq, Wk, bk,
                     nc.tensor.transpose(x_bank[duo, c][:, j, u, :], words[:, j, 256 * c + u : 256 * (c + 1) : 2], ident[:])
 
         def group_x(duo, c, engine):
-            x_grouped[duo, c] = work.tile([P, 2 * P * PACK], BF16, name="x_grouped", bufs=6, align_bytes=64)
+            x_grouped[duo, c] = work.tile([P, 2 * P * PACK], BF16, name="x_grouped", bufs=4, align_bytes=64)
             copy_on(
                 engine,
                 x_grouped[duo, c][:].bitcast(F32).rearrange("p (j r u) -> p j r u", j=2, u=2),
@@ -136,12 +138,13 @@ def tile_qwen2vlattention_pa_kernel(tc, hidden_states, cos, sin, Wq, bq, Wk, bk,
                 out=x_codes[half, c][:, cols].bitcast(E5M2X4), scales=x_scales[half, c][:, cols], in_=x_grouped[duo, c][:]
             )
 
-        def group_w(pair, c, engine):
-            w_grouped[pair, c] = work.tile([P, PAIR_W * PACK], BF16, name="w_grouped", bufs=5, align_bytes=64)
+        def group_w(pair, c, engine, cols=slice(0, PAIR_W)):
+            if cols.start == 0:
+                w_grouped[pair, c] = work.tile([P, PAIR_W * PACK], BF16, name="w_grouped", bufs=6, align_bytes=64)
             copy_on(
                 engine,
-                w_grouped[pair, c][:].rearrange("p (n i t) -> p n t i", i=4, t=PACK),
-                w_raw[pair, c].rearrange("p t (n i) -> p n t i", i=4),
+                w_grouped[pair, c][:, cols.start * PACK : cols.stop * PACK].rearrange("p (n i t) -> p n t i", i=4, t=PACK),
+                w_raw[pair, c][:, :, cols].rearrange("p t (n i) -> p n t i", i=4),
             )
 
         def quantize_w(pair, c):
@@ -149,26 +152,26 @@ def tile_qwen2vlattention_pa_kernel(tc, hidden_states, cos, sin, Wq, bq, Wk, bk,
             w_scales[pair, c] = keep.tile([P, PAIR_W], U8, name="w_scales%d_%d" % (pair, c), align_bytes=64)
             nc.vector.quantize_mx(out=w_codes[pair, c][:].bitcast(E4M3X4), scales=w_scales[pair, c][:], in_=w_grouped[pair, c][:])
 
-        def project(pair, half):
+        def project(pair, half, pass_major=False):
             for h in range(2):
                 sums[pair, half, h] = psum.tile([P, HALF_TOK], F32, name="sums", tag="mx%d" % half)
+            steps = [(h, c) for h in range(2) for c in range(PASSES)]
+            for h, c in sorted(steps, key=lambda s: s[1]) if pass_major else steps:
                 cols = slice(h * DH, (h + 1) * DH)
-                for c in range(PASSES):
-                    nc.tensor.matmul_mx(
-                        out=sums[pair, half, h][:],
-                        lhsT=w_codes[pair, c][:, cols].bitcast(E4M3X4),
-                        lhsT_scale=w_scales[pair, c][:, cols],
-                        rhs=x_codes[half, c][:].bitcast(E5M2X4),
-                        rhs_scale=x_scales[half, c][:],
-                        start=(c == 0),
-                        stop=(c == PASSES - 1),
-                    )
+                nc.tensor.matmul_mx(
+                    out=sums[pair, half, h][:],
+                    lhsT=w_codes[pair, c][:, cols].bitcast(E4M3X4),
+                    lhsT_scale=w_scales[pair, c][:, cols],
+                    rhs=x_codes[half, c][:].bitcast(E5M2X4),
+                    rhs_scale=x_scales[half, c][:],
+                    start=(c == 0),
+                    stop=(c == PASSES - 1),
+                )
 
         def bias_col(pair, h):
-            col = PAIR_W + 2 * pair + h
-            return bias_sb[:, col : col + 1]
+            return bias_cols[:, 2 * pair + h : 2 * pair + h + 1]
 
-        def store(pair, tiles, src):
+        def store(pair, half, cols=slice(0, PAIR_W)):
             if pair == 0:
                 dst, col0 = out_1, 0
             elif pair == V_PAIR:
@@ -176,15 +179,21 @@ def tile_qwen2vlattention_pa_kernel(tc, hidden_states, cos, sin, Wq, bq, Wk, bk,
             else:
                 dst, col0 = out_0, (pair - 1) * PAIR_W
             rows = dst[0].rearrange("(t p) h d -> p t (h d)", p=P)
-            nc.sync.dma_start(out=rows[:, tiles, col0 : col0 + PAIR_W], in_=src)
+            nc.sync.dma_start(out=rows[:, half * TILES : (half + 1) * TILES, col0 + cols.start : col0 + cols.stop], in_=results[pair, half][:, :, cols])
+
+        def turn_table(k, table, tag):
+            bank = psum.tile([P, TILES, P], BF16, name="table_bank", tag=tag)
+            for t in range(TILES):
+                nc.tensor.transpose(bank[:, t, :], table[:, t, :], ident_bf[:])
+            tables_chan[k] = keep.tile([P, HALF_TOK], BF16, name="table_chan%d" % k)
+            nc.scalar.copy(out=tables_chan[k][:], in_=bank[:].rearrange("p t r -> p (t r)"))
 
         def multiply_chan(pair):
             for h in range(2):
-                cos_part[pair, 0, h] = work.tile([P, HALF_TOK], F32, name="cos_chan")
-                sin_part[pair, 0, h] = work.tile([P, HALF_TOK], F32, name="sin_chan")
-                for part, k in ((cos_part, 0), (sin_part, 1)):
+                for k, parts in enumerate((cos_part, sin_part)):
+                    parts[pair, h] = work.tile([P, HALF_TOK], F32, name="part_chan%d" % k)
                     nc.vector.scalar_tensor_tensor(
-                        out=part[pair, 0, h][:], in0=sums[pair, 0, h][:], scalar=bias_col(pair, h), in1=tables_chan[:, k, :], op0=ADD, op1=MULT
+                        out=parts[pair, h][:], in0=sums[pair, 0, h][:], scalar=bias_col(pair, h), in1=tables_chan[k][:], op0=ADD, op1=MULT
                     )
 
         def turn_and_add(pair):
@@ -192,148 +201,140 @@ def tile_qwen2vlattention_pa_kernel(tc, hidden_states, cos, sin, Wq, bq, Wk, bk,
                 turned[pair, 0, h] = psum.tile([P, TILES, DH], F32, name="turned", tag="tr0")
                 for t in range(TILES):
                     toks = slice(t * P, (t + 1) * P)
-                    nc.tensor.matmul(turned[pair, 0, h][:, t, :], lhsT=cos_part[pair, 0, h][:, toks], rhs=ident[:], is_transpose=True, start=True, stop=False)
-                    nc.tensor.matmul(turned[pair, 0, h][:, t, :], lhsT=sin_part[pair, 0, h][:, toks], rhs=swap[:], is_transpose=True, start=False, stop=True)
+                    nc.tensor.matmul(turned[pair, 0, h][:, t, :], lhsT=cos_part[pair, h][:, toks], rhs=ident[:], is_transpose=True, start=True, stop=False)
+                    nc.tensor.matmul(turned[pair, 0, h][:, t, :], lhsT=sin_part[pair, h][:, toks], rhs=swap[:], is_transpose=True, start=False, stop=True)
 
-        def finish_chan(pair):
-            result[pair, 0] = work.tile([P, TILES, PAIR_W], F32, name="result0")
+        def copy_out(pair, half, engines=("scalar", "scalar")):
+            results[pair, half] = work.tile([P, TILES, PAIR_W], F32, name="result_copied")
             for h in range(2):
-                nc.scalar.copy(out=result[pair, 0][:, :, h * DH : (h + 1) * DH], in_=turned[pair, 0, h][:])
-            store(pair, slice(0, TILES), result[pair, 0][:])
+                copy_on(engines[h], results[pair, half][:, :, h * DH : (h + 1) * DH], turned[pair, half, h][:])
 
-        def add_bias(pair):
+        def add_bias(pair, half):
             for h in range(2):
-                biased[pair, h] = work.tile([P, HALF_TOK], F32, name="biased", bufs=4)
-                nc.scalar.activation(out=biased[pair, h][:], in_=sums[pair, 1, h][:], func=IDENTITY, bias=bias_col(pair, h))
+                biased[pair, half, h] = work.tile([P, HALF_TOK], F32, name="biased", bufs=4)
+                nc.scalar.activation(out=biased[pair, half, h][:], in_=sums[pair, half, h][:], func=IDENTITY, bias=bias_col(pair, h))
 
-        def turn(pair):
+        def turn(pair, half, tag):
             for h in range(2):
-                turned[pair, 1, h] = psum.tile([P, TILES, DH], F32, name="turned", tag="tr1")
+                turned[pair, half, h] = psum.tile([P, TILES, DH], F32, name="turned", tag=tag)
                 for t in range(TILES):
-                    nc.tensor.transpose(turned[pair, 1, h][:, t, :], biased[pair, h][:, t * P : (t + 1) * P], ident[:])
+                    nc.tensor.transpose(turned[pair, half, h][:, t, :], biased[pair, half, h][:, t * P : (t + 1) * P], ident[:])
 
-        def rotate_tok(pair):
-            result[pair, 1] = work.tile([P, TILES, PAIR_W], F32, name="result1")
+        def rotate_tok(pair, half, adders=(nc.gpsimd, nc.gpsimd)):
+            result = work.tile([P, TILES, PAIR_W], F32, name="result_added")
+            results[pair, half] = result
             for h in range(2):
-                u = turned[pair, 1, h]
-                cos_part[pair, 1, h] = work.tile([P, TILES, DH], F32, name="cos_tokp")
-                sin_part[pair, 1, h] = work.tile([P, TILES, DH], F32, name="sin_tokp")
-                nc.vector.tensor_tensor(out=cos_part[pair, 1, h][:], in0=u[:], in1=cos_tok[1][:], op=MULT)
-                nc.vector.tensor_tensor(out=sin_part[pair, 1, h][:, :, 0:HALF_D], in0=u[:, :, HALF_D:DH], in1=sin_tok[1][:, :, 0:HALF_D], op=MULT)
-                nc.vector.tensor_tensor(out=sin_part[pair, 1, h][:, :, HALF_D:DH], in0=u[:, :, 0:HALF_D], in1=sin_tok[1][:, :, HALF_D:DH], op=MULT)
-                nc.gpsimd.tensor_tensor(out=result[pair, 1][:, :, h * DH : (h + 1) * DH], in0=cos_part[pair, 1, h][:], in1=sin_part[pair, 1, h][:], op=ADD)
-            store(pair, slice(TILES, 2 * TILES), result[pair, 1][:])
+                u = turned[pair, half, h]
+                cos_u = work.tile([P, TILES, DH], F32, name="cos_u")
+                sin_u = work.tile([P, TILES, DH], F32, name="sin_u")
+                nc.vector.tensor_tensor(out=cos_u[:], in0=u[:], in1=cos_tok[half][:], op=MULT)
+                nc.vector.tensor_tensor(out=sin_u[:, :, 0:HALF_D], in0=u[:, :, HALF_D:DH], in1=sin_tok[half][:, :, 0:HALF_D], op=MULT)
+                nc.vector.tensor_tensor(out=sin_u[:, :, HALF_D:DH], in0=u[:, :, 0:HALF_D], in1=sin_tok[half][:, :, HALF_D:DH], op=MULT)
+                adders[h].tensor_tensor(out=result[:, :, h * DH : (h + 1) * DH], in0=cos_u[:], in1=sin_u[:], op=ADD)
 
-        def project_v(duo):
-            half = duo // 2
-            sums[V_PAIR, duo] = psum.tile([P, 2, PAIR_W], F32, name="sums_v", tag="mx%d" % half)
-            for j in range(2):
-                t = (duo % 2) * 2 + j
-                toks = slice(t * P, (t + 1) * P)
-                for c in range(PASSES):
-                    nc.tensor.matmul_mx(
-                        out=sums[V_PAIR, duo][:, j, :],
-                        lhsT=x_codes[half, c][:, toks].bitcast(E5M2X4),
-                        lhsT_scale=x_scales[half, c][:, toks],
-                        rhs=w_codes[V_PAIR, c][:].bitcast(E4M3X4),
-                        rhs_scale=w_scales[V_PAIR, c][:],
-                        start=(c == 0),
-                        stop=(c == PASSES - 1),
-                    )
+        def negate_low_sin(half):
+            low = sin_tok[half][:, :, 0:HALF_D]
+            nc.vector.tensor_scalar(out=low, in0=low, scalar1=-1.0, scalar2=None, op0=MULT)
 
-        def finish_v(duo):
-            res = work.tile([P, 2, PAIR_W], F32, name="result_v", bufs=4)
-            nc.vector.tensor_tensor(
-                out=res[:], in0=sums[V_PAIR, duo][:], in1=bias_sb[:, 0:PAIR_W].unsqueeze(1).to_broadcast([P, 2, PAIR_W]), op=ADD
-            )
-            store(V_PAIR, slice(2 * duo, 2 * duo + 2), res[:])
+        bias_bank = psum.tile([P, HEADS], F32, tag="mx0")
+        nc.tensor.matmul(bias_bank[:], lhsT=bias_rows[:], rhs=ident_bf[:, 0:HEADS], start=True, stop=True)
+        bias_cols = keep.tile([P, HEADS], F32)
+        nc.scalar.activation(out=bias_cols[:], in_=bias_bank[:], func=IDENTITY)
 
-        for c, tag in enumerate(("mx1", "tr0", "tr1")):
-            transpose_x(0, c, tag)
-        group_x(0, 0, "vector")
-        group_x(0, 1, "scalar")
-        group_x(0, 2, "vector")
-        for c, tag in enumerate(("mx1", "tr0", "tr1")):
-            transpose_x(1, c, tag)
-            group_x(1, c, "scalar")
+        tags = ("mx0", "mx1", "tr0", "tr1")
+        for duo in range(4):
+            for c in range(PASSES):
+                transpose_x(duo, c, tags[(duo * PASSES + c) % 4])
+        for duo in range(2):
+            group_x(duo, 0, "scalar")
+            group_x(duo, 1, "vector")
+            group_x(duo, 2, "scalar")
+            for c in range(PASSES):
+                quantize_x(duo, c)
         for c in range(PASSES):
-            quantize_x(0, c)
+            group_x(2, c, "scalar")
+        group_x(3, 0, "scalar")
+        quantize_x(2, 0)
+        quantize_x(2, 1)
         group_w(0, 0, "vector")
-        group_w(0, 1, "vector")
+        quantize_x(2, 2)
         quantize_w(0, 0)
-        quantize_x(1, 0)
+        group_w(0, 1, "scalar")
         group_w(0, 2, "vector")
         quantize_w(0, 1)
-        quantize_x(1, 1)
         quantize_w(0, 2)
-        quantize_x(1, 2)
-
-        bias_bank = psum.tile([P, PAIR_W + BV_ROW], F32, tag="mx1")
-        nc.tensor.matmul(bias_bank[:, 0:PAIR_W], lhsT=ident_bf[:, BV_ROW : BV_ROW + 1].to_broadcast([P, P]), rhs=bias_rows[:], start=True, stop=True)
-        nc.tensor.matmul(bias_bank[:, PAIR_W : PAIR_W + BV_ROW], lhsT=bias_rows[:, 0:DH], rhs=ident_bf[:, 0:BV_ROW], start=True, stop=True)
-        bias_sb = keep.tile([P, PAIR_W + BV_ROW], F32)
-        nc.scalar.activation(out=bias_sb[:], in_=bias_bank[:], func=IDENTITY)
-
-        project(0, 0)
-
-        sin_swapped = keep.tile([P, TILES, DH], BF16)
-        nc.vector.tensor_copy(out=sin_swapped[:, :, 0:HALF_D], in_=sin_tok[0][:, :, HALF_D:DH])
-        nc.vector.tensor_scalar(out=sin_swapped[:, :, HALF_D:DH], in0=sin_tok[0][:, :, 0:HALF_D], scalar1=-1.0, scalar2=None, op0=MULT)
-        table_bank = psum.tile([P, 2, TILES, P], BF16, tag="tr0")
-        for k, table in enumerate((cos_tok[0], sin_swapped)):
-            for t in range(TILES):
-                nc.tensor.transpose(table_bank[:, k, t, :], table[:, t, :], ident_bf[:])
-        tables_chan = keep.tile([P, 2, HALF_TOK], BF16)
-        nc.scalar.copy(out=tables_chan[:], in_=table_bank[:].rearrange("p k t r -> p k (t r)"))
-
-        multiply_chan(0)
-        for duo in (2, 3):
-            for c, tag in enumerate(("tr1", "mx1", "tr0")):
-                transpose_x(duo, c, tag)
-                group_x(duo, c, "scalar")
-        for c in range(PASSES):
-            quantize_x(2, c)
-        group_w(1, 0, "vector")
+        project(0, 0, pass_major=True)
+        group_x(3, 1, "scalar")
+        group_x(3, 2, "scalar")
         for c in range(PASSES):
             quantize_x(3, c)
-        turn_and_add(0)
         project(0, 1)
-        group_w(1, 1, "scalar")
-        quantize_w(1, 0)
+        add_bias(0, 0)
+        group_w(1, 0, "vector")
+        negate_low_sin(0)
+        group_w(1, 1, "vector")
+        sin_swapped = keep.tile([P, TILES, DH], BF16)
+        nc.vector.tensor_copy(out=sin_swapped[:, :, 0:HALF_D], in_=sin_tok[0][:, :, HALF_D:DH])
+        nc.vector.tensor_copy(out=sin_swapped[:, :, HALF_D:DH], in_=sin_tok[0][:, :, 0:HALF_D])
         group_w(1, 2, "vector")
-        quantize_w(1, 1)
-        nc.vector.tensor_scalar(out=sin_tok[1][:, :, 0:HALF_D], in0=sin_tok[1][:, :, 0:HALF_D], scalar1=-1.0, scalar2=None, op0=MULT)
-        quantize_w(1, 2)
-        group_w(2, 0, "vector")
+        for c in range(PASSES):
+            quantize_w(1, c)
+        turn(0, 0, "tr0")
+        add_bias(0, 1)
+        turn_table(1, sin_swapped, "tr1")
+        turn_table(0, cos_tok[0], "tr1")
+        rotate_tok(0, 0)
+        group_w(2, 0, "scalar")
         group_w(2, 1, "scalar")
-        add_bias(0)
-
-        last = ROPE_PAIRS - 1
-        for pair in range(1, ROPE_PAIRS):
+        order = (1, 2, 3, 4, 5, V_PAIR, 6)
+        for r in range(5):
+            pair = order[r]
             project(pair, 0)
-            finish_chan(pair - 1)
+            if pair > 1:
+                copy_out(pair - 1, 0)
+                store(pair - 2, 1)
+            store(pair - 1, 0)
             multiply_chan(pair)
             project(pair, 1)
-            group_w(pair + 1, 2, "scalar")
+            group_w(order[r + 1], 2, "scalar", slice(0, SCALAR_COLS))
+            group_w(order[r + 1], 2, "vector", slice(SCALAR_COLS, PAIR_W))
+            if pair == 1:
+                negate_low_sin(1)
             for c in range(PASSES):
-                quantize_w(pair + 1, c)
-            add_bias(pair)
-            turn(pair - 1)
-            rotate_tok(pair - 1)
-            if pair < last:
-                turn_and_add(pair)
-                group_w(pair + 2, 0, "scalar")
-                group_w(pair + 2, 1, "scalar")
-
-        project_v(0)
-        project_v(1)
+                quantize_w(order[r + 1], c)
+            add_bias(pair, 1)
+            turn(pair - 1, 1, "tr1")
+            rotate_tok(pair - 1, 1)
+            turn_and_add(pair)
+            group_w(order[r + 2], 0, "scalar")
+            group_w(order[r + 2], 1, "scalar")
+        last = V_PAIR - 1
+        project(V_PAIR, 0)
+        copy_out(last - 1, 0)
+        store(last - 1, 0)
+        store(last - 2, 1)
+        group_w(last, 2, "vector")
+        for c in range(PASSES):
+            quantize_w(last, c)
+        add_bias(V_PAIR, 0)
+        project(V_PAIR, 1)
+        add_bias(V_PAIR, 1)
+        turn(last - 1, 1, "tr1")
+        rotate_tok(last - 1, 1)
+        turn(V_PAIR, 0, "tr0")
+        copy_out(V_PAIR, 0)
+        store(V_PAIR, 0)
+        project(last, 0)
+        multiply_chan(last)
+        project(last, 1)
+        add_bias(last, 1)
+        store(last - 1, 1)
+        turn(V_PAIR, 1, "tr0")
+        copy_out(V_PAIR, 1)
+        store(V_PAIR, 1)
+        turn(last, 1, "tr1")
+        rotate_tok(last, 1, (nc.gpsimd, nc.vector))
         turn_and_add(last)
-        finish_v(0)
-        finish_v(1)
-        finish_chan(last)
-        turn(last)
-        project_v(2)
-        project_v(3)
-        rotate_tok(last)
-        finish_v(2)
-        finish_v(3)
+        copy_out(last, 0)
+        store(last, 0)
+        store(last, 1)

@@ -67,6 +67,11 @@ def tile_qwen2vlattention_pa_kernel(tc, hidden_states, cos, sin, Wq, bq, Wk, bk,
 
         for duo in range(4):
             load_x(duo)
+        bias_rows = keep.tile([P, DH], BF16)
+        nc.vector.memset(bias_rows[:], 0.0)
+        nc.sync.dma_start(out=bias_rows[0:KV_HEADS, :], in_=bk)
+        nc.sync.dma_start(out=bias_rows[KV_HEADS : KV_HEADS + Q_HEADS, :], in_=bq)
+        nc.sync.dma_start(out=bias_rows[KV_HEADS + Q_HEADS : HEADS, :], in_=bv)
         load_w(Wk, 0, 1, 0)
         load_table(sin, sin_tok, "sin", 0)
         load_w(Wq, 1, 1, 0)
@@ -78,16 +83,10 @@ def tile_qwen2vlattention_pa_kernel(tc, hidden_states, cos, sin, Wq, bq, Wk, bk,
         load_w(Wq, 5, 2, 4 * PAIR_W)
         load_w(Wv, V_PAIR, 1, 0)
 
-        bias_rows = keep.tile([P, DH], BF16)
-        nc.vector.memset(bias_rows[:], 0.0)
-        nc.scalar.dma_start(out=bias_rows[0:KV_HEADS, :], in_=bk)
-        nc.scalar.dma_start(out=bias_rows[KV_HEADS : KV_HEADS + Q_HEADS, :], in_=bq)
-        nc.scalar.dma_start(out=bias_rows[KV_HEADS + Q_HEADS : HEADS, :], in_=bv)
-
         ident = keep.tile([P, P], F32)
         make_identity(nc, ident[:])
         ident_bf = keep.tile([P, P], BF16)
-        make_identity(nc, ident_bf[:])
+        nc.scalar.activation(out=ident_bf[:], in_=ident[:], func=IDENTITY)
         swap = keep.tile([P, P], F32)
         nc.gpsimd.tensor_copy(out=swap[:, 0:HALF_D], in_=ident[:, HALF_D:P])
         nc.gpsimd.tensor_copy(out=swap[:, HALF_D:P], in_=ident[:, 0:HALF_D])
@@ -236,10 +235,6 @@ def tile_qwen2vlattention_pa_kernel(tc, hidden_states, cos, sin, Wq, bq, Wk, bk,
             low = sin_tok[half][:, :, 0:HALF_D]
             nc.vector.tensor_scalar(out=low, in0=low, scalar1=-1.0, scalar2=None, op0=MULT)
 
-        bias_bank = psum.tile([P, HEADS], F32, tag="mx0")
-        nc.tensor.matmul(bias_bank[:], lhsT=bias_rows[:], rhs=ident_bf[:, 0:HEADS], start=True, stop=True)
-        bias_cols = keep.tile([P, HEADS], F32)
-        nc.scalar.activation(out=bias_cols[:], in_=bias_bank[:], func=IDENTITY)
 
         tags = ("mx0", "mx1", "tr0", "tr1")
         for duo in range(4):
@@ -254,6 +249,8 @@ def tile_qwen2vlattention_pa_kernel(tc, hidden_states, cos, sin, Wq, bq, Wk, bk,
         for c in range(PASSES):
             group_x(2, c, "scalar")
         group_x(3, 0, "scalar")
+        bias_bank = psum.tile([P, HEADS], F32, tag="mx1")
+        nc.tensor.matmul(bias_bank[:], lhsT=bias_rows[:], rhs=ident_bf[:, 0:HEADS], start=True, stop=True)
         quantize_x(2, 0)
         quantize_x(2, 1)
         group_w(0, 0, "vector")
@@ -263,6 +260,8 @@ def tile_qwen2vlattention_pa_kernel(tc, hidden_states, cos, sin, Wq, bq, Wk, bk,
         group_w(0, 2, "vector")
         quantize_w(0, 1)
         quantize_w(0, 2)
+        bias_cols = keep.tile([P, HEADS], F32)
+        nc.vector.tensor_copy(out=bias_cols[:], in_=bias_bank[:])
         project(0, 0, pass_major=True)
         group_x(3, 1, "scalar")
         group_x(3, 2, "scalar")

@@ -27,9 +27,12 @@ HALF_TOK = TILES * P
 PAIR_W = 2 * DH
 ROPE_PAIRS = (Q_HEADS + KV_HEADS) // 2
 V_PAIR = ROPE_PAIRS
+K_PAIR = 0
+JOINED = ((1, 3), (1,))
+RB = 3
 SECTIONS = ((0, 32), (32, 80), (80, 128))
 HEADS = Q_HEADS + 2 * KV_HEADS
-SCALAR_COLS = 192
+SCALAR_COLS = 160
 
 
 def tile_qwen2vlattention_pa_kernel(tc, hidden_states, cos, sin, Wq, bq, Wk, bk, Wv, bv, out_0, out_1, out_2):
@@ -41,7 +44,7 @@ def tile_qwen2vlattention_pa_kernel(tc, hidden_states, cos, sin, Wq, bq, Wk, bk,
         psum = ctx.enter_context(tc.psum_pool(name="psum", bufs=2))
         ctx.enter_context(tc.manual_schedule())
 
-        x_hbm = hidden_states[0].rearrange("(t p) m -> p t m", p=P)
+        x_hbm = hidden_states[0].rearrange("(half p t) m -> p half t m", p=P, t=TILES)
         x_raw = {}
         w_raw = {}
         cos_tok = {}
@@ -49,7 +52,7 @@ def tile_qwen2vlattention_pa_kernel(tc, hidden_states, cos, sin, Wq, bq, Wk, bk,
 
         def load_x(duo):
             x_raw[duo] = keep.tile([P, 2, M], BF16, name="x_raw%d" % duo)
-            nc.sync.dma_start(out=x_raw[duo][:], in_=x_hbm[:, 2 * duo : 2 * duo + 2, :])
+            nc.sync.dma_start(out=x_raw[duo][:], in_=x_hbm[:, duo // 2, 2 * (duo % 2) : 2 * (duo % 2) + 2, :])
 
         def load_w(w_hbm, first_pair, pairs, col0):
             rows = w_hbm.rearrange("(c p j) h d -> c p j (h d)", p=P, j=PACK)
@@ -62,8 +65,8 @@ def tile_qwen2vlattention_pa_kernel(tc, hidden_states, cos, sin, Wq, bq, Wk, bk,
         def load_table(table, tok, label, half):
             tok[half] = keep.tile([P, TILES, DH], BF16, name="%s_tok%d" % (label, half))
             for comp, (d0, d1) in enumerate(SECTIONS):
-                rows = table[comp][0].rearrange("(t p) d -> p t d", p=P)
-                nc.sync.dma_start(out=tok[half][:, :, d0:d1], in_=rows[:, TILES * half : TILES * (half + 1), d0:d1])
+                rows = table[comp][0].rearrange("(half p t) d -> p half t d", p=P, t=TILES)
+                nc.sync.dma_start(out=tok[half][:, :, d0:d1], in_=rows[:, half, :, d0:d1])
 
         for duo in range(4):
             load_x(duo)
@@ -72,16 +75,14 @@ def tile_qwen2vlattention_pa_kernel(tc, hidden_states, cos, sin, Wq, bq, Wk, bk,
         nc.sync.dma_start(out=bias_rows[0:KV_HEADS, :], in_=bk)
         nc.sync.dma_start(out=bias_rows[KV_HEADS : KV_HEADS + Q_HEADS, :], in_=bq)
         nc.sync.dma_start(out=bias_rows[KV_HEADS + Q_HEADS : HEADS, :], in_=bv)
-        load_w(Wk, 0, 1, 0)
-        load_table(sin, sin_tok, "sin", 0)
-        load_w(Wq, 1, 1, 0)
+        load_w(Wk, K_PAIR, 1, 0)
         load_table(cos, cos_tok, "cos", 0)
-        load_w(Wq, 2, 1, PAIR_W)
+        load_table(sin, sin_tok, "sin", 0)
+        load_w(Wv, V_PAIR, 1, 0)
+        load_w(Wq, 1, 2, 0)
         load_table(cos, cos_tok, "cos", 1)
         load_table(sin, sin_tok, "sin", 1)
         load_w(Wq, 3, 2, 2 * PAIR_W)
-        load_w(Wq, 5, 2, 4 * PAIR_W)
-        load_w(Wv, V_PAIR, 1, 0)
 
         ident = keep.tile([P, P], F32)
         make_identity(nc, ident[:])
@@ -109,6 +110,8 @@ def tile_qwen2vlattention_pa_kernel(tc, hidden_states, cos, sin, Wq, bq, Wk, bk,
         turned = {}
         tables_chan = {}
         results = {}
+        products = {}
+        added = {}
 
         def copy_on(engine, out, in_):
             if engine == "scalar":
@@ -139,7 +142,7 @@ def tile_qwen2vlattention_pa_kernel(tc, hidden_states, cos, sin, Wq, bq, Wk, bk,
 
         def group_w(pair, c, engine, cols=slice(0, PAIR_W)):
             if cols.start == 0:
-                w_grouped[pair, c] = work.tile([P, PAIR_W * PACK], BF16, name="w_grouped", bufs=6, align_bytes=64)
+                w_grouped[pair, c] = work.tile([P, PAIR_W * PACK], BF16, name="w_grouped", bufs=5, align_bytes=64)
             copy_on(
                 engine,
                 w_grouped[pair, c][:, cols.start * PACK : cols.stop * PACK].rearrange("p (n i t) -> p n t i", i=4, t=PACK),
@@ -151,34 +154,51 @@ def tile_qwen2vlattention_pa_kernel(tc, hidden_states, cos, sin, Wq, bq, Wk, bk,
             w_scales[pair, c] = keep.tile([P, PAIR_W], U8, name="w_scales%d_%d" % (pair, c), align_bytes=64)
             nc.vector.quantize_mx(out=w_codes[pair, c][:].bitcast(E4M3X4), scales=w_scales[pair, c][:], in_=w_grouped[pair, c][:])
 
-        def project(pair, half, pass_major=False):
+        def open_sums(pair, half):
             for h in range(2):
                 sums[pair, half, h] = psum.tile([P, HALF_TOK], F32, name="sums", tag="mx%d" % half)
-            steps = [(h, c) for h in range(2) for c in range(PASSES)]
-            for h, c in sorted(steps, key=lambda s: s[1]) if pass_major else steps:
-                cols = slice(h * DH, (h + 1) * DH)
-                nc.tensor.matmul_mx(
-                    out=sums[pair, half, h][:],
-                    lhsT=w_codes[pair, c][:, cols].bitcast(E4M3X4),
-                    lhsT_scale=w_scales[pair, c][:, cols],
-                    rhs=x_codes[half, c][:].bitcast(E5M2X4),
-                    rhs_scale=x_scales[half, c][:],
-                    start=(c == 0),
-                    stop=(c == PASSES - 1),
-                )
+
+        def multiply_pass(pair, half, h, c):
+            cols = slice(h * DH, (h + 1) * DH)
+            nc.tensor.matmul_mx(
+                out=sums[pair, half, h][:],
+                lhsT=w_codes[pair, c][:, cols].bitcast(E4M3X4),
+                lhsT_scale=w_scales[pair, c][:, cols],
+                rhs=x_codes[half, c][:].bitcast(E5M2X4),
+                rhs_scale=x_scales[half, c][:],
+                start=(c == 0),
+                stop=(c == PASSES - 1),
+            )
+
+        def project(pair, half):
+            open_sums(pair, half)
+            for h in range(2):
+                for c in range(PASSES):
+                    multiply_pass(pair, half, h, c)
+
+        def project_by_pass(pair, halves):
+            for half in halves:
+                open_sums(pair, half)
+            for c in range(PASSES):
+                for half in halves:
+                    for h in range(2):
+                        multiply_pass(pair, half, h, c)
 
         def bias_col(pair, h):
             return bias_cols[:, 2 * pair + h : 2 * pair + h + 1]
 
-        def store(pair, half, cols=slice(0, PAIR_W)):
-            if pair == 0:
-                dst, col0 = out_1, 0
-            elif pair == V_PAIR:
-                dst, col0 = out_2, 0
-            else:
-                dst, col0 = out_0, (pair - 1) * PAIR_W
-            rows = dst[0].rearrange("(t p) h d -> p t (h d)", p=P)
-            nc.sync.dma_start(out=rows[:, half * TILES : (half + 1) * TILES, col0 + cols.start : col0 + cols.stop], in_=results[pair, half][:, :, cols])
+        def result_cols(pair, half, name):
+            first = pair - 1 if pair - 1 in JOINED[half] else pair
+            if pair == first:
+                results[first, half] = work.tile([P, TILES, (2 if pair in JOINED[half] else 1) * PAIR_W], F32, name=name, bufs=RB)
+            return results[first, half][:, :, (pair - first) * PAIR_W : (pair - first + 1) * PAIR_W]
+
+        def store(first, half):
+            dst = {K_PAIR: out_1, V_PAIR: out_2}.get(first, out_0)
+            col0 = 0 if first in (K_PAIR, V_PAIR) else (first - 1) * PAIR_W
+            src = results[first, half]
+            rows = dst[0].rearrange("(half p t) h d -> p half t (h d)", p=P, t=TILES)
+            nc.sync.dma_start(out=rows[:, half, :, col0 : col0 + src.shape[2]], in_=src[:])
 
         def turn_table(k, table, tag):
             bank = psum.tile([P, TILES, P], BF16, name="table_bank", tag=tag)
@@ -204,13 +224,13 @@ def tile_qwen2vlattention_pa_kernel(tc, hidden_states, cos, sin, Wq, bq, Wk, bk,
                     nc.tensor.matmul(turned[pair, 0, h][:, t, :], lhsT=sin_part[pair, h][:, toks], rhs=swap[:], is_transpose=True, start=False, stop=True)
 
         def copy_out(pair, half, engines=("scalar", "scalar")):
-            results[pair, half] = work.tile([P, TILES, PAIR_W], F32, name="result_copied")
+            result = result_cols(pair, half, "result_copied")
             for h in range(2):
-                copy_on(engines[h], results[pair, half][:, :, h * DH : (h + 1) * DH], turned[pair, half, h][:])
+                copy_on(engines[h], result[:, :, h * DH : (h + 1) * DH], turned[pair, half, h][:])
 
         def add_bias(pair, half):
             for h in range(2):
-                biased[pair, half, h] = work.tile([P, HALF_TOK], F32, name="biased", bufs=4)
+                biased[pair, half, h] = work.tile([P, HALF_TOK], F32, name="biased", bufs=6)
                 nc.scalar.activation(out=biased[pair, half, h][:], in_=sums[pair, half, h][:], func=IDENTITY, bias=bias_col(pair, h))
 
         def turn(pair, half, tag):
@@ -219,17 +239,25 @@ def tile_qwen2vlattention_pa_kernel(tc, hidden_states, cos, sin, Wq, bq, Wk, bk,
                 for t in range(TILES):
                     nc.tensor.transpose(turned[pair, half, h][:, t, :], biased[pair, half, h][:, t * P : (t + 1) * P], ident[:])
 
-        def rotate_tok(pair, half, adders=(nc.gpsimd, nc.gpsimd)):
-            result = work.tile([P, TILES, PAIR_W], F32, name="result_added")
-            results[pair, half] = result
+        def multiply_tok(pair, half, h):
+            u = turned[pair, half, h]
+            cos_u = work.tile([P, TILES, DH], F32, name="cos_u")
+            sin_u = work.tile([P, TILES, DH], F32, name="sin_u")
+            nc.vector.tensor_tensor(out=cos_u[:], in0=u[:], in1=cos_tok[half][:], op=MULT)
+            nc.vector.tensor_tensor(out=sin_u[:, :, 0:HALF_D], in0=u[:, :, HALF_D:DH], in1=sin_tok[half][:, :, 0:HALF_D], op=MULT)
+            nc.vector.tensor_tensor(out=sin_u[:, :, HALF_D:DH], in0=u[:, :, 0:HALF_D], in1=sin_tok[half][:, :, HALF_D:DH], op=MULT)
+            products[pair, half, h] = (cos_u, sin_u)
+
+        def add_tok(pair, half, h, engine):
+            cos_u, sin_u = products[pair, half, h]
+            if h == 0:
+                added[pair, half] = result_cols(pair, half, "result_added")
+            engine.tensor_tensor(out=added[pair, half][:, :, h * DH : (h + 1) * DH], in0=cos_u[:], in1=sin_u[:], op=ADD)
+
+        def rotate_tok(pair, half):
             for h in range(2):
-                u = turned[pair, half, h]
-                cos_u = work.tile([P, TILES, DH], F32, name="cos_u")
-                sin_u = work.tile([P, TILES, DH], F32, name="sin_u")
-                nc.vector.tensor_tensor(out=cos_u[:], in0=u[:], in1=cos_tok[half][:], op=MULT)
-                nc.vector.tensor_tensor(out=sin_u[:, :, 0:HALF_D], in0=u[:, :, HALF_D:DH], in1=sin_tok[half][:, :, 0:HALF_D], op=MULT)
-                nc.vector.tensor_tensor(out=sin_u[:, :, HALF_D:DH], in0=u[:, :, 0:HALF_D], in1=sin_tok[half][:, :, HALF_D:DH], op=MULT)
-                adders[h].tensor_tensor(out=result[:, :, h * DH : (h + 1) * DH], in0=cos_u[:], in1=sin_u[:], op=ADD)
+                multiply_tok(pair, half, h)
+                add_tok(pair, half, h, nc.gpsimd)
 
         def negate_low_sin(half):
             low = sin_tok[half][:, :, 0:HALF_D]
@@ -262,78 +290,91 @@ def tile_qwen2vlattention_pa_kernel(tc, hidden_states, cos, sin, Wq, bq, Wk, bk,
         quantize_w(0, 2)
         bias_cols = keep.tile([P, HEADS], F32)
         nc.vector.tensor_copy(out=bias_cols[:], in_=bias_bank[:])
-        project(0, 0, pass_major=True)
+        project_by_pass(K_PAIR, (0,))
         group_x(3, 1, "scalar")
         group_x(3, 2, "scalar")
         for c in range(PASSES):
             quantize_x(3, c)
         project(0, 1)
         add_bias(0, 0)
-        group_w(1, 0, "vector")
         negate_low_sin(0)
-        group_w(1, 1, "vector")
         sin_swapped = keep.tile([P, TILES, DH], BF16)
         nc.vector.tensor_copy(out=sin_swapped[:, :, 0:HALF_D], in_=sin_tok[0][:, :, HALF_D:DH])
         nc.vector.tensor_copy(out=sin_swapped[:, :, HALF_D:DH], in_=sin_tok[0][:, :, 0:HALF_D])
-        group_w(1, 2, "vector")
-        for c in range(PASSES):
-            quantize_w(1, c)
-        turn(0, 0, "tr0")
-        add_bias(0, 1)
-        turn_table(1, sin_swapped, "tr1")
+        turn(K_PAIR, 0, "tr0")
+        add_bias(K_PAIR, 1)
         turn_table(0, cos_tok[0], "tr1")
-        rotate_tok(0, 0)
+        turn_table(1, sin_swapped, "tr1")
+        group_w(V_PAIR, 0, "vector")
+        group_w(V_PAIR, 1, "vector")
+        quantize_w(V_PAIR, 0)
+        group_w(V_PAIR, 2, "vector")
+        quantize_w(V_PAIR, 1)
+        quantize_w(V_PAIR, 2)
+        project_by_pass(V_PAIR, (0,))
+        multiply_tok(K_PAIR, 0, 0)
+        add_tok(K_PAIR, 0, 0, nc.gpsimd)
+        multiply_tok(K_PAIR, 0, 1)
+        group_w(1, 0, "scalar")
+        add_bias(V_PAIR, 0)
+        project(V_PAIR, 1)
+        add_bias(V_PAIR, 1)
+        group_w(1, 1, "vector")
+        quantize_w(1, 0)
+        group_w(1, 2, "vector")
+        quantize_w(1, 1)
+        quantize_w(1, 2)
+        add_tok(K_PAIR, 0, 1, nc.vector)
+        turn(V_PAIR, 0, "tr0")
+        turn(V_PAIR, 1, "tr1")
         group_w(2, 0, "scalar")
+        copy_out(V_PAIR, 1, ("scalar", "scalar"))
         group_w(2, 1, "scalar")
-        order = (1, 2, 3, 4, 5, V_PAIR, 6)
-        for r in range(5):
-            pair = order[r]
+        store(K_PAIR, 0)
+        store(V_PAIR, 1)
+        late = {2: (Wq, 5, 2, 4 * PAIR_W)}
+        last = V_PAIR - 1
+        stores = {1: [], 2: [(V_PAIR, 0), (K_PAIR, 1)], 3: [(1, 0)], 4: [(1, 1)], 5: [(3, 0), (3, 1)]}
+        for pair in range(1, last):
             project(pair, 0)
             if pair > 1:
                 copy_out(pair - 1, 0)
-                store(pair - 2, 1)
-            store(pair - 1, 0)
+            for first, half in stores[pair]:
+                store(first, half)
+            if pair in late:
+                load_w(*late[pair])
             multiply_chan(pair)
             project(pair, 1)
-            group_w(order[r + 1], 2, "scalar", slice(0, SCALAR_COLS))
-            group_w(order[r + 1], 2, "vector", slice(SCALAR_COLS, PAIR_W))
-            if pair == 1:
-                negate_low_sin(1)
+            group_w(pair + 1, 2, "scalar", slice(0, SCALAR_COLS))
+            group_w(pair + 1, 2, "vector", slice(SCALAR_COLS, PAIR_W))
             for c in range(PASSES):
-                quantize_w(order[r + 1], c)
+                quantize_w(pair + 1, c)
+            if pair == 1:
+                copy_out(V_PAIR, 0)
+                negate_low_sin(1)
             add_bias(pair, 1)
             turn(pair - 1, 1, "tr1")
             rotate_tok(pair - 1, 1)
             turn_and_add(pair)
-            group_w(order[r + 2], 0, "scalar")
-            group_w(order[r + 2], 1, "scalar")
-        last = V_PAIR - 1
-        project(V_PAIR, 0)
+            if pair + 2 <= last:
+                group_w(pair + 2, 0, "scalar")
+                group_w(pair + 2, 1, "scalar")
+        project(last, 0)
         copy_out(last - 1, 0)
         store(last - 1, 0)
         store(last - 2, 1)
-        group_w(last, 2, "vector")
-        for c in range(PASSES):
-            quantize_w(last, c)
-        add_bias(V_PAIR, 0)
-        project(V_PAIR, 1)
-        add_bias(V_PAIR, 1)
+        multiply_chan(last)
         turn(last - 1, 1, "tr1")
         rotate_tok(last - 1, 1)
-        turn(V_PAIR, 0, "tr0")
-        copy_out(V_PAIR, 0)
-        store(V_PAIR, 0)
-        project(last, 0)
-        multiply_chan(last)
         project(last, 1)
         add_bias(last, 1)
-        store(last - 1, 1)
-        turn(V_PAIR, 1, "tr0")
-        copy_out(V_PAIR, 1)
-        store(V_PAIR, 1)
-        turn(last, 1, "tr1")
-        rotate_tok(last, 1, (nc.gpsimd, nc.vector))
         turn_and_add(last)
+        turn(last, 1, "mx0")
         copy_out(last, 0)
         store(last, 0)
+        store(last - 1, 1)
+        multiply_tok(last, 1, 0)
+        add_tok(last, 1, 0, nc.gpsimd)
+        multiply_tok(last, 1, 1)
+        add_tok(last, 1, 1, nc.vector)
         store(last, 1)

@@ -5,8 +5,9 @@ from concourse.masks import make_identity
 
 S, M, DH = 1024, 1536, 128
 Q_HEADS, KV_HEADS = 12, 2
-FLOPS = 2 * S * M * (Q_HEADS + 2 * KV_HEADS) * DH
-BYTES = 2 * (S * M + (M + 1) * (Q_HEADS + 2 * KV_HEADS) * DH + 2 * S * DH) + 4 * S * (Q_HEADS + 2 * KV_HEADS) * DH
+HEADS = Q_HEADS + 2 * KV_HEADS
+FLOPS = 2 * S * M * HEADS * DH
+BYTES = 2 * (S * M + (M + 1) * HEADS * DH + 2 * S * DH) + 4 * S * HEADS * DH
 
 F32 = mybir.dt.float32
 BF16 = mybir.dt.bfloat16
@@ -21,18 +22,22 @@ IDENTITY = mybir.ActivationFunctionType.Identity
 P = 128
 PACK = 4
 PASSES = M // (P * PACK)
-HALF_D = DH // 2
+PASS_WORDS = P * PACK // 2
+LOW, HIGH = slice(0, DH // 2), slice(DH // 2, DH)
 TILES = 4
 HALF_TOK = TILES * P
+DUO = 2
+DUOS = S // (DUO * P)
 PAIR_W = 2 * DH
-ROPE_PAIRS = (Q_HEADS + KV_HEADS) // 2
-V_PAIR = ROPE_PAIRS
-K_PAIR = 0
-JOINED = ((1, 3), (1,))
-RB = 3
+K_PAIR, V_PAIR = 0, 1 + Q_HEADS // 2
+LAST_Q = V_PAIR - 1
 SECTIONS = ((0, 32), (32, 80), (80, 128))
-HEADS = Q_HEADS + 2 * KV_HEADS
+RUN = 4
+
+JOINED = ((1, 3), (1,))
 SCALAR_COLS = 160
+SHARED_ROUNDS = 3
+LATE_LOAD_ROUND = 2
 
 
 def tile_qwen2vlattention_pa_kernel(tc, hidden_states, cos, sin, Wq, bq, Wk, bk, Wv, bv, out_0, out_1, out_2):
@@ -51,8 +56,9 @@ def tile_qwen2vlattention_pa_kernel(tc, hidden_states, cos, sin, Wq, bq, Wk, bk,
         sin_tok = {}
 
         def load_x(duo):
-            x_raw[duo] = keep.tile([P, 2, M], BF16, name="x_raw%d" % duo)
-            nc.sync.dma_start(out=x_raw[duo][:], in_=x_hbm[:, duo // 2, 2 * (duo % 2) : 2 * (duo % 2) + 2, :])
+            first = DUO * (duo % 2)
+            x_raw[duo] = keep.tile([P, DUO, M], BF16, name="x_raw%d" % duo)
+            nc.sync.dma_start(out=x_raw[duo][:], in_=x_hbm[:, duo // 2, first : first + DUO, :])
 
         def load_w(w_hbm, first_pair, pairs, col0):
             rows = w_hbm.rearrange("(c p j) h d -> c p j (h d)", p=P, j=PACK)
@@ -62,13 +68,16 @@ def tile_qwen2vlattention_pa_kernel(tc, hidden_states, cos, sin, Wq, bq, Wk, bk,
                 for s in range(pairs):
                     w_raw[first_pair + s, c] = raw[:, :, s * PAIR_W : (s + 1) * PAIR_W]
 
+        def load_two_query_pairs(first_pair):
+            load_w(Wq, first_pair, 2, (first_pair - 1) * PAIR_W)
+
         def load_table(table, tok, label, half):
             tok[half] = keep.tile([P, TILES, DH], BF16, name="%s_tok%d" % (label, half))
             for comp, (d0, d1) in enumerate(SECTIONS):
                 rows = table[comp][0].rearrange("(half p t) d -> p half t d", p=P, t=TILES)
                 nc.sync.dma_start(out=tok[half][:, :, d0:d1], in_=rows[:, half, :, d0:d1])
 
-        for duo in range(4):
+        for duo in range(DUOS):
             load_x(duo)
         bias_rows = keep.tile([P, DH], BF16)
         nc.vector.memset(bias_rows[:], 0.0)
@@ -79,18 +88,18 @@ def tile_qwen2vlattention_pa_kernel(tc, hidden_states, cos, sin, Wq, bq, Wk, bk,
         load_table(cos, cos_tok, "cos", 0)
         load_table(sin, sin_tok, "sin", 0)
         load_w(Wv, V_PAIR, 1, 0)
-        load_w(Wq, 1, 2, 0)
+        load_two_query_pairs(1)
         load_table(cos, cos_tok, "cos", 1)
         load_table(sin, sin_tok, "sin", 1)
-        load_w(Wq, 3, 2, 2 * PAIR_W)
+        load_two_query_pairs(3)
 
         ident = keep.tile([P, P], F32)
         make_identity(nc, ident[:])
         ident_bf = keep.tile([P, P], BF16)
         nc.scalar.activation(out=ident_bf[:], in_=ident[:], func=IDENTITY)
         swap = keep.tile([P, P], F32)
-        nc.gpsimd.tensor_copy(out=swap[:, 0:HALF_D], in_=ident[:, HALF_D:P])
-        nc.gpsimd.tensor_copy(out=swap[:, HALF_D:P], in_=ident[:, 0:HALF_D])
+        nc.gpsimd.tensor_copy(out=swap[:, LOW], in_=ident[:, HIGH])
+        nc.gpsimd.tensor_copy(out=swap[:, HIGH], in_=ident[:, LOW])
 
         x_codes = {}
         x_scales = {}
@@ -104,49 +113,40 @@ def tile_qwen2vlattention_pa_kernel(tc, hidden_states, cos, sin, Wq, bq, Wk, bk,
         w_codes = {}
         w_scales = {}
         sums = {}
-        cos_part = {}
-        sin_part = {}
+        chan_products = {}
+        tok_products = {}
         biased = {}
         turned = {}
         tables_chan = {}
         results = {}
-        products = {}
         added = {}
 
-        def copy_on(engine, out, in_):
-            if engine == "scalar":
-                nc.scalar.copy(out=out, in_=in_)
-            else:
-                nc.vector.tensor_copy(out=out, in_=in_)
-
         def transpose_x(duo, c, tag):
-            x_bank[duo, c] = psum.tile([P, 2, 2, P], F32, name="x_bank", tag=tag)
+            x_bank[duo, c] = psum.tile([P, DUO, 2, P], F32, name="x_bank", tag=tag)
             words = x_raw[duo][:].bitcast(F32)
-            for j in range(2):
+            for j in range(DUO):
                 for u in range(2):
-                    nc.tensor.transpose(x_bank[duo, c][:, j, u, :], words[:, j, 256 * c + u : 256 * (c + 1) : 2], ident[:])
+                    nc.tensor.transpose(x_bank[duo, c][:, j, u, :], words[:, j, PASS_WORDS * c + u : PASS_WORDS * (c + 1) : 2], ident[:])
 
-        def group_x(duo, c, engine):
-            x_grouped[duo, c] = work.tile([P, 2 * P * PACK], BF16, name="x_grouped", bufs=4, align_bytes=64)
-            copy_on(
-                engine,
-                x_grouped[duo, c][:].bitcast(F32).rearrange("p (j r u) -> p j r u", j=2, u=2),
-                x_bank[duo, c][:].rearrange("p j u r -> p j r u"),
+        def group_x(duo, c, copy):
+            x_grouped[duo, c] = work.tile([P, DUO * P * PACK], BF16, name="x_grouped", bufs=4, align_bytes=64)
+            copy(
+                out=x_grouped[duo, c][:].bitcast(F32).rearrange("p (j r u) -> p j r u", j=DUO, u=2),
+                in_=x_bank[duo, c][:].rearrange("p j u r -> p j r u"),
             )
 
         def quantize_x(duo, c):
-            half, cols = duo // 2, slice((duo % 2) * 2 * P, (duo % 2 + 1) * 2 * P)
+            half, cols = duo // 2, slice((duo % 2) * DUO * P, (duo % 2 + 1) * DUO * P)
             nc.vector.quantize_mx(
                 out=x_codes[half, c][:, cols].bitcast(E5M2X4), scales=x_scales[half, c][:, cols], in_=x_grouped[duo, c][:]
             )
 
-        def group_w(pair, c, engine, cols=slice(0, PAIR_W)):
+        def group_w(pair, c, copy, cols=slice(0, PAIR_W)):
             if cols.start == 0:
                 w_grouped[pair, c] = work.tile([P, PAIR_W * PACK], BF16, name="w_grouped", bufs=5, align_bytes=64)
-            copy_on(
-                engine,
-                w_grouped[pair, c][:, cols.start * PACK : cols.stop * PACK].rearrange("p (n i t) -> p n t i", i=4, t=PACK),
-                w_raw[pair, c][:, :, cols].rearrange("p t (n i) -> p n t i", i=4),
+            copy(
+                out=w_grouped[pair, c][:, cols.start * PACK : cols.stop * PACK].rearrange("p (n i t) -> p n t i", i=RUN, t=PACK),
+                in_=w_raw[pair, c][:, :, cols].rearrange("p t (n i) -> p n t i", i=RUN),
             )
 
         def quantize_w(pair, c):
@@ -154,79 +154,83 @@ def tile_qwen2vlattention_pa_kernel(tc, hidden_states, cos, sin, Wq, bq, Wk, bk,
             w_scales[pair, c] = keep.tile([P, PAIR_W], U8, name="w_scales%d_%d" % (pair, c), align_bytes=64)
             nc.vector.quantize_mx(out=w_codes[pair, c][:].bitcast(E4M3X4), scales=w_scales[pair, c][:], in_=w_grouped[pair, c][:])
 
-        def open_sums(pair, half):
+        by_head = [(h, c) for h in range(2) for c in range(PASSES)]
+        by_pass = [(h, c) for c in range(PASSES) for h in range(2)]
+
+        def project(pair, half, steps):
             for h in range(2):
                 sums[pair, half, h] = psum.tile([P, HALF_TOK], F32, name="sums", tag="mx%d" % half)
-
-        def multiply_pass(pair, half, h, c):
-            cols = slice(h * DH, (h + 1) * DH)
-            nc.tensor.matmul_mx(
-                out=sums[pair, half, h][:],
-                lhsT=w_codes[pair, c][:, cols].bitcast(E4M3X4),
-                lhsT_scale=w_scales[pair, c][:, cols],
-                rhs=x_codes[half, c][:].bitcast(E5M2X4),
-                rhs_scale=x_scales[half, c][:],
-                start=(c == 0),
-                stop=(c == PASSES - 1),
-            )
-
-        def project(pair, half):
-            open_sums(pair, half)
-            for h in range(2):
-                for c in range(PASSES):
-                    multiply_pass(pair, half, h, c)
-
-        def project_by_pass(pair, halves):
-            for half in halves:
-                open_sums(pair, half)
-            for c in range(PASSES):
-                for half in halves:
-                    for h in range(2):
-                        multiply_pass(pair, half, h, c)
+            for h, c in steps:
+                cols = slice(h * DH, (h + 1) * DH)
+                nc.tensor.matmul_mx(
+                    out=sums[pair, half, h][:],
+                    lhsT=w_codes[pair, c][:, cols].bitcast(E4M3X4),
+                    lhsT_scale=w_scales[pair, c][:, cols],
+                    rhs=x_codes[half, c][:].bitcast(E5M2X4),
+                    rhs_scale=x_scales[half, c][:],
+                    start=(c == 0),
+                    stop=(c == PASSES - 1),
+                )
 
         def bias_col(pair, h):
             return bias_cols[:, 2 * pair + h : 2 * pair + h + 1]
 
+        def first_of(pair, half):
+            return pair - 1 if pair - 1 in JOINED[half] else pair
+
         def result_cols(pair, half, name):
-            first = pair - 1 if pair - 1 in JOINED[half] else pair
+            first = first_of(pair, half)
             if pair == first:
-                results[first, half] = work.tile([P, TILES, (2 if pair in JOINED[half] else 1) * PAIR_W], F32, name=name, bufs=RB)
+                results[first, half] = work.tile([P, TILES, (2 if pair in JOINED[half] else 1) * PAIR_W], F32, name=name)
             return results[first, half][:, :, (pair - first) * PAIR_W : (pair - first + 1) * PAIR_W]
 
-        def store(first, half):
-            dst = {K_PAIR: out_1, V_PAIR: out_2}.get(first, out_0)
-            col0 = 0 if first in (K_PAIR, V_PAIR) else (first - 1) * PAIR_W
-            src = results[first, half]
-            rows = dst[0].rearrange("(half p t) h d -> p half t (h d)", p=P, t=TILES)
-            nc.sync.dma_start(out=rows[:, half, :, col0 : col0 + src.shape[2]], in_=src[:])
+        def store(pair, half):
+            if pair not in JOINED[half]:
+                first = first_of(pair, half)
+                dst = {K_PAIR: out_1, V_PAIR: out_2}.get(first, out_0)
+                col0 = 0 if first in (K_PAIR, V_PAIR) else (first - 1) * PAIR_W
+                src = results[first, half]
+                rows = dst[0].rearrange("(half p t) h d -> p half t (h d)", p=P, t=TILES)
+                nc.sync.dma_start(out=rows[:, half, :, col0 : col0 + src.shape[2]], in_=src[:])
 
-        def turn_table(k, table, tag):
+        def copy_out(pair, half):
+            result = result_cols(pair, half, "result_copied")
+            for h in range(2):
+                nc.scalar.copy(out=result[:, :, h * DH : (h + 1) * DH], in_=turned[pair, half, h][:])
+
+        def negate_low_sin(half):
+            low = sin_tok[half][:, :, LOW]
+            nc.vector.tensor_scalar(out=low, in0=low, scalar1=-1.0, scalar2=None, op0=MULT)
+
+        def turn_table(which, table, tag):
             bank = psum.tile([P, TILES, P], BF16, name="table_bank", tag=tag)
             for t in range(TILES):
                 nc.tensor.transpose(bank[:, t, :], table[:, t, :], ident_bf[:])
-            tables_chan[k] = keep.tile([P, HALF_TOK], BF16, name="table_chan%d" % k)
-            nc.scalar.copy(out=tables_chan[k][:], in_=bank[:].rearrange("p t r -> p (t r)"))
+            tables_chan[which] = keep.tile([P, HALF_TOK], BF16, name="table_chan%d" % which)
+            nc.scalar.copy(out=tables_chan[which][:], in_=bank[:].rearrange("p t r -> p (t r)"))
 
         def multiply_chan(pair):
             for h in range(2):
-                for k, parts in enumerate((cos_part, sin_part)):
-                    parts[pair, h] = work.tile([P, HALF_TOK], F32, name="part_chan%d" % k)
+                for which in range(2):
+                    product = work.tile([P, HALF_TOK], F32, name="part_chan%d" % which)
+                    chan_products[pair, h, which] = product
                     nc.vector.scalar_tensor_tensor(
-                        out=parts[pair, h][:], in0=sums[pair, 0, h][:], scalar=bias_col(pair, h), in1=tables_chan[k][:], op0=ADD, op1=MULT
+                        out=product[:], in0=sums[pair, 0, h][:], scalar=bias_col(pair, h), in1=tables_chan[which][:], op0=ADD, op1=MULT
                     )
 
         def turn_and_add(pair):
             for h in range(2):
                 turned[pair, 0, h] = psum.tile([P, TILES, DH], F32, name="turned", tag="tr0")
                 for t in range(TILES):
-                    toks = slice(t * P, (t + 1) * P)
-                    nc.tensor.matmul(turned[pair, 0, h][:, t, :], lhsT=cos_part[pair, h][:, toks], rhs=ident[:], is_transpose=True, start=True, stop=False)
-                    nc.tensor.matmul(turned[pair, 0, h][:, t, :], lhsT=sin_part[pair, h][:, toks], rhs=swap[:], is_transpose=True, start=False, stop=True)
-
-        def copy_out(pair, half, engines=("scalar", "scalar")):
-            result = result_cols(pair, half, "result_copied")
-            for h in range(2):
-                copy_on(engines[h], result[:, :, h * DH : (h + 1) * DH], turned[pair, half, h][:])
+                    for which, moving in enumerate((ident, swap)):
+                        nc.tensor.matmul(
+                            turned[pair, 0, h][:, t, :],
+                            lhsT=chan_products[pair, h, which][:, t * P : (t + 1) * P],
+                            rhs=moving[:],
+                            is_transpose=True,
+                            start=(which == 0),
+                            stop=(which == 1),
+                        )
 
         def add_bias(pair, half):
             for h in range(2):
@@ -244,12 +248,12 @@ def tile_qwen2vlattention_pa_kernel(tc, hidden_states, cos, sin, Wq, bq, Wk, bk,
             cos_u = work.tile([P, TILES, DH], F32, name="cos_u")
             sin_u = work.tile([P, TILES, DH], F32, name="sin_u")
             nc.vector.tensor_tensor(out=cos_u[:], in0=u[:], in1=cos_tok[half][:], op=MULT)
-            nc.vector.tensor_tensor(out=sin_u[:, :, 0:HALF_D], in0=u[:, :, HALF_D:DH], in1=sin_tok[half][:, :, 0:HALF_D], op=MULT)
-            nc.vector.tensor_tensor(out=sin_u[:, :, HALF_D:DH], in0=u[:, :, 0:HALF_D], in1=sin_tok[half][:, :, HALF_D:DH], op=MULT)
-            products[pair, half, h] = (cos_u, sin_u)
+            nc.vector.tensor_tensor(out=sin_u[:, :, LOW], in0=u[:, :, HIGH], in1=sin_tok[half][:, :, LOW], op=MULT)
+            nc.vector.tensor_tensor(out=sin_u[:, :, HIGH], in0=u[:, :, LOW], in1=sin_tok[half][:, :, HIGH], op=MULT)
+            tok_products[pair, half, h] = (cos_u, sin_u)
 
         def add_tok(pair, half, h, engine):
-            cos_u, sin_u = products[pair, half, h]
+            cos_u, sin_u = tok_products[pair, half, h]
             if h == 0:
                 added[pair, half] = result_cols(pair, half, "result_added")
             engine.tensor_tensor(out=added[pair, half][:, :, h * DH : (h + 1) * DH], in0=cos_u[:], in1=sin_u[:], op=ADD)
@@ -259,122 +263,123 @@ def tile_qwen2vlattention_pa_kernel(tc, hidden_states, cos, sin, Wq, bq, Wk, bk,
                 multiply_tok(pair, half, h)
                 add_tok(pair, half, h, nc.gpsimd)
 
-        def negate_low_sin(half):
-            low = sin_tok[half][:, :, 0:HALF_D]
-            nc.vector.tensor_scalar(out=low, in0=low, scalar1=-1.0, scalar2=None, op0=MULT)
-
+        on_scalar, on_vector = nc.scalar.copy, nc.vector.tensor_copy
 
         tags = ("mx0", "mx1", "tr0", "tr1")
-        for duo in range(4):
+        for duo in range(DUOS):
             for c in range(PASSES):
-                transpose_x(duo, c, tags[(duo * PASSES + c) % 4])
+                transpose_x(duo, c, tags[(duo * PASSES + c) % len(tags)])
         for duo in range(2):
-            group_x(duo, 0, "scalar")
-            group_x(duo, 1, "vector")
-            group_x(duo, 2, "scalar")
+            for c, copy in enumerate((on_scalar, on_vector, on_scalar)):
+                group_x(duo, c, copy)
             for c in range(PASSES):
                 quantize_x(duo, c)
         for c in range(PASSES):
-            group_x(2, c, "scalar")
-        group_x(3, 0, "scalar")
+            group_x(2, c, on_scalar)
+        group_x(3, 0, on_scalar)
         bias_bank = psum.tile([P, HEADS], F32, tag="mx1")
         nc.tensor.matmul(bias_bank[:], lhsT=bias_rows[:], rhs=ident_bf[:, 0:HEADS], start=True, stop=True)
         quantize_x(2, 0)
         quantize_x(2, 1)
-        group_w(0, 0, "vector")
+        group_w(K_PAIR, 0, on_vector)
         quantize_x(2, 2)
-        quantize_w(0, 0)
-        group_w(0, 1, "scalar")
-        group_w(0, 2, "vector")
-        quantize_w(0, 1)
-        quantize_w(0, 2)
+        quantize_w(K_PAIR, 0)
+        group_w(K_PAIR, 1, on_scalar)
+        group_w(K_PAIR, 2, on_vector)
+        quantize_w(K_PAIR, 1)
+        quantize_w(K_PAIR, 2)
         bias_cols = keep.tile([P, HEADS], F32)
         nc.vector.tensor_copy(out=bias_cols[:], in_=bias_bank[:])
-        project_by_pass(K_PAIR, (0,))
-        group_x(3, 1, "scalar")
-        group_x(3, 2, "scalar")
+
+        project(K_PAIR, 0, by_pass)
+        group_x(3, 1, on_scalar)
+        group_x(3, 2, on_scalar)
         for c in range(PASSES):
             quantize_x(3, c)
-        project(0, 1)
-        add_bias(0, 0)
+        project(K_PAIR, 1, by_head)
+        add_bias(K_PAIR, 0)
         negate_low_sin(0)
         sin_swapped = keep.tile([P, TILES, DH], BF16)
-        nc.vector.tensor_copy(out=sin_swapped[:, :, 0:HALF_D], in_=sin_tok[0][:, :, HALF_D:DH])
-        nc.vector.tensor_copy(out=sin_swapped[:, :, HALF_D:DH], in_=sin_tok[0][:, :, 0:HALF_D])
+        nc.vector.tensor_copy(out=sin_swapped[:, :, LOW], in_=sin_tok[0][:, :, HIGH])
+        nc.vector.tensor_copy(out=sin_swapped[:, :, HIGH], in_=sin_tok[0][:, :, LOW])
         turn(K_PAIR, 0, "tr0")
         add_bias(K_PAIR, 1)
         turn_table(0, cos_tok[0], "tr1")
         turn_table(1, sin_swapped, "tr1")
-        group_w(V_PAIR, 0, "vector")
-        group_w(V_PAIR, 1, "vector")
+
+        group_w(V_PAIR, 0, on_vector)
+        group_w(V_PAIR, 1, on_vector)
         quantize_w(V_PAIR, 0)
-        group_w(V_PAIR, 2, "vector")
+        group_w(V_PAIR, 2, on_vector)
         quantize_w(V_PAIR, 1)
         quantize_w(V_PAIR, 2)
-        project_by_pass(V_PAIR, (0,))
+        project(V_PAIR, 0, by_pass)
         multiply_tok(K_PAIR, 0, 0)
         add_tok(K_PAIR, 0, 0, nc.gpsimd)
         multiply_tok(K_PAIR, 0, 1)
-        group_w(1, 0, "scalar")
+        group_w(1, 0, on_scalar)
         add_bias(V_PAIR, 0)
-        project(V_PAIR, 1)
+        project(V_PAIR, 1, by_head)
         add_bias(V_PAIR, 1)
-        group_w(1, 1, "vector")
+        group_w(1, 1, on_vector)
         quantize_w(1, 0)
-        group_w(1, 2, "vector")
+        group_w(1, 2, on_vector)
         quantize_w(1, 1)
         quantize_w(1, 2)
         add_tok(K_PAIR, 0, 1, nc.vector)
         turn(V_PAIR, 0, "tr0")
         turn(V_PAIR, 1, "tr1")
-        group_w(2, 0, "scalar")
-        copy_out(V_PAIR, 1, ("scalar", "scalar"))
-        group_w(2, 1, "scalar")
+        group_w(2, 0, on_scalar)
+        copy_out(V_PAIR, 1)
+        group_w(2, 1, on_scalar)
         store(K_PAIR, 0)
         store(V_PAIR, 1)
-        late = {2: (Wq, 5, 2, 4 * PAIR_W)}
-        last = V_PAIR - 1
-        stores = {1: [], 2: [(V_PAIR, 0), (K_PAIR, 1)], 3: [(1, 0)], 4: [(1, 1)], 5: [(3, 0), (3, 1)]}
-        for pair in range(1, last):
-            project(pair, 0)
+
+        for pair in range(1, LAST_Q):
+            project(pair, 0, by_head)
             if pair > 1:
                 copy_out(pair - 1, 0)
-            for first, half in stores[pair]:
-                store(first, half)
-            if pair in late:
-                load_w(*late[pair])
+                store(pair - 1, 0)
+                store(pair - 2, 1)
+            if pair == LATE_LOAD_ROUND:
+                load_two_query_pairs(LAST_Q - 1)
             multiply_chan(pair)
-            project(pair, 1)
-            group_w(pair + 1, 2, "scalar", slice(0, SCALAR_COLS))
-            group_w(pair + 1, 2, "vector", slice(SCALAR_COLS, PAIR_W))
+            project(pair, 1, by_head)
+            if pair <= SHARED_ROUNDS:
+                group_w(pair + 1, 2, on_scalar, slice(0, SCALAR_COLS))
+                group_w(pair + 1, 2, on_vector, slice(SCALAR_COLS, PAIR_W))
+            else:
+                group_w(pair + 1, 2, on_scalar)
             for c in range(PASSES):
                 quantize_w(pair + 1, c)
             if pair == 1:
                 copy_out(V_PAIR, 0)
+                store(V_PAIR, 0)
                 negate_low_sin(1)
             add_bias(pair, 1)
             turn(pair - 1, 1, "tr1")
             rotate_tok(pair - 1, 1)
             turn_and_add(pair)
-            if pair + 2 <= last:
-                group_w(pair + 2, 0, "scalar")
-                group_w(pair + 2, 1, "scalar")
-        project(last, 0)
-        copy_out(last - 1, 0)
-        store(last - 1, 0)
-        store(last - 2, 1)
-        multiply_chan(last)
-        turn(last - 1, 1, "tr1")
-        rotate_tok(last - 1, 1)
-        project(last, 1)
-        add_bias(last, 1)
-        turn_and_add(last)
-        turn(last, 1, "mx0")
-        copy_out(last, 0)
-        store(last, 0)
-        store(last - 1, 1)
-        multiply_tok(last, 1, 0)
-        add_tok(last, 1, 0, nc.gpsimd)
-        multiply_tok(last, 1, 1)
-        add_tok(last, 1, 1, nc.vector)
-        store(last, 1)
+            if pair + 2 <= LAST_Q:
+                group_w(pair + 2, 0, on_scalar)
+                group_w(pair + 2, 1, on_scalar)
+
+        project(LAST_Q, 0, by_head)
+        copy_out(LAST_Q - 1, 0)
+        store(LAST_Q - 1, 0)
+        store(LAST_Q - 2, 1)
+        multiply_chan(LAST_Q)
+        turn(LAST_Q - 1, 1, "tr1")
+        rotate_tok(LAST_Q - 1, 1)
+        project(LAST_Q, 1, by_head)
+        add_bias(LAST_Q, 1)
+        turn_and_add(LAST_Q)
+        turn(LAST_Q, 1, "mx0")
+        copy_out(LAST_Q, 0)
+        store(LAST_Q, 0)
+        store(LAST_Q - 1, 1)
+        multiply_tok(LAST_Q, 1, 0)
+        add_tok(LAST_Q, 1, 0, nc.gpsimd)
+        multiply_tok(LAST_Q, 1, 1)
+        add_tok(LAST_Q, 1, 1, nc.vector)
+        store(LAST_Q, 1)

from contextlib import ExitStack

import concourse.mybir as mybir
from concourse.masks import make_identity

S, M, DH = 1024, 1536, 128
Q_HEADS, KV_HEADS = 12, 2
HEADS = Q_HEADS + 2 * KV_HEADS
FLOPS = 2 * S * M * HEADS * DH
BYTES = 2 * (S * M + (M + 1) * HEADS * DH + 2 * S * DH) + 4 * S * HEADS * DH

F32 = mybir.dt.float32
BF16 = mybir.dt.bfloat16
U32 = mybir.dt.uint32
U8 = mybir.dt.uint8
E4M3X4 = mybir.dt.float8_e4m3fn_x4
E5M2X4 = mybir.dt.float8_e5m2_x4
ADD = mybir.AluOpType.add
MULT = mybir.AluOpType.mult
IDENTITY = mybir.ActivationFunctionType.Identity

P = 128
PACK = 4
PASSES = M // (P * PACK)
PASS_WORDS = P * PACK // 2
LOW, HIGH = slice(0, DH // 2), slice(DH // 2, DH)
TILES = 4
HALF_TOK = TILES * P
DUO = 2
DUOS = S // (DUO * P)
PAIR_W = 2 * DH
K_PAIR, V_PAIR = 0, 1 + Q_HEADS // 2
LAST_Q = V_PAIR - 1
SECTIONS = ((0, 32), (32, 80), (80, 128))
RUN = 4

JOINED = ((1, 3), (1,))
SCALAR_COLS = 160
SHARED_ROUNDS = 3
LATE_LOAD_ROUND = 2


def tile_qwen2vlattention_pa_kernel(tc, hidden_states, cos, sin, Wq, bq, Wk, bk, Wv, bv, out_0, out_1, out_2):
    nc = tc.nc

    with ExitStack() as ctx:
        keep = ctx.enter_context(tc.tile_pool(name="keep", bufs=1))
        work = ctx.enter_context(tc.tile_pool(name="work", bufs=3))
        psum = ctx.enter_context(tc.psum_pool(name="psum", bufs=2))
        ctx.enter_context(tc.manual_schedule())

        x_hbm = hidden_states[0].rearrange("(half p t) m -> p half t m", p=P, t=TILES)
        x_raw = {}
        w_raw = {}
        cos_tok = {}
        sin_tok = {}

        def load_x(duo):
            first = DUO * (duo % 2)
            x_raw[duo] = keep.tile([P, DUO, M], BF16, name="x_raw%d" % duo)
            nc.sync.dma_start(out=x_raw[duo][:], in_=x_hbm[:, duo // 2, first : first + DUO, :])

        def load_w(w_hbm, first_pair, pairs, col0):
            rows = w_hbm.rearrange("(c p j) h d -> c p j (h d)", p=P, j=PACK)
            for c in range(PASSES):
                raw = keep.tile([P, PACK, pairs * PAIR_W], BF16, name="w_raw%d_%d" % (first_pair, c))
                nc.sync.dma_start(out=raw[:], in_=rows[c][:, :, col0 : col0 + pairs * PAIR_W])
                for s in range(pairs):
                    w_raw[first_pair + s, c] = raw[:, :, s * PAIR_W : (s + 1) * PAIR_W]

        def load_two_query_pairs(first_pair):
            load_w(Wq, first_pair, 2, (first_pair - 1) * PAIR_W)

        def load_table(table, tok, label, half):
            tok[half] = keep.tile([P, TILES, DH], BF16, name="%s_tok%d" % (label, half))
            for comp, (d0, d1) in enumerate(SECTIONS):
                rows = table[comp][0].rearrange("(half p t) d -> p half t d", p=P, t=TILES)
                nc.sync.dma_start(out=tok[half][:, :, d0:d1], in_=rows[:, half, :, d0:d1])

        for duo in range(DUOS):
            load_x(duo)
        bias_rows = keep.tile([P, DH], BF16)
        nc.vector.memset(bias_rows[:], 0.0)
        nc.sync.dma_start(out=bias_rows[0:KV_HEADS, :], in_=bk)
        nc.sync.dma_start(out=bias_rows[KV_HEADS : KV_HEADS + Q_HEADS, :], in_=bq)
        nc.sync.dma_start(out=bias_rows[KV_HEADS + Q_HEADS : HEADS, :], in_=bv)
        load_w(Wk, K_PAIR, 1, 0)
        load_table(cos, cos_tok, "cos", 0)
        load_table(sin, sin_tok, "sin", 0)
        load_w(Wv, V_PAIR, 1, 0)
        load_two_query_pairs(1)
        load_table(cos, cos_tok, "cos", 1)
        load_table(sin, sin_tok, "sin", 1)
        load_two_query_pairs(3)

        ident = keep.tile([P, P], F32)
        make_identity(nc, ident[:])
        ident_bf = keep.tile([P, P], BF16)
        nc.scalar.activation(out=ident_bf[:], in_=ident[:], func=IDENTITY)
        swap = keep.tile([P, P], F32)
        nc.gpsimd.tensor_copy(out=swap[:, LOW], in_=ident[:, HIGH])
        nc.gpsimd.tensor_copy(out=swap[:, HIGH], in_=ident[:, LOW])

        x_codes = {}
        x_scales = {}
        for half in range(2):
            for c in range(PASSES):
                x_codes[half, c] = keep.tile([P, HALF_TOK], U32, name="x_codes%d_%d" % (half, c), align_bytes=64)
                x_scales[half, c] = keep.tile([P, HALF_TOK], U8, name="x_scales%d_%d" % (half, c), align_bytes=64)
        x_bank = {}
        x_grouped = {}
        w_grouped = {}
        w_codes = {}
        w_scales = {}
        sums = {}
        chan_products = {}
        tok_products = {}
        biased = {}
        turned = {}
        tables_chan = {}
        results = {}
        added = {}

        def transpose_x(duo, c, tag):
            x_bank[duo, c] = psum.tile([P, DUO, 2, P], F32, name="x_bank", tag=tag)
            words = x_raw[duo][:].bitcast(F32)
            for j in range(DUO):
                for u in range(2):
                    nc.tensor.transpose(x_bank[duo, c][:, j, u, :], words[:, j, PASS_WORDS * c + u : PASS_WORDS * (c + 1) : 2], ident[:])

        def group_x(duo, c, copy):
            x_grouped[duo, c] = work.tile([P, DUO * P * PACK], BF16, name="x_grouped", bufs=4, align_bytes=64)
            copy(
                out=x_grouped[duo, c][:].bitcast(F32).rearrange("p (j r u) -> p j r u", j=DUO, u=2),
                in_=x_bank[duo, c][:].rearrange("p j u r -> p j r u"),
            )

        def quantize_x(duo, c):
            half, cols = duo // 2, slice((duo % 2) * DUO * P, (duo % 2 + 1) * DUO * P)
            nc.vector.quantize_mx(
                out=x_codes[half, c][:, cols].bitcast(E5M2X4), scales=x_scales[half, c][:, cols], in_=x_grouped[duo, c][:]
            )

        def group_w(pair, c, copy, cols=slice(0, PAIR_W)):
            if cols.start == 0:
                w_grouped[pair, c] = work.tile([P, PAIR_W * PACK], BF16, name="w_grouped", bufs=5, align_bytes=64)
            copy(
                out=w_grouped[pair, c][:, cols.start * PACK : cols.stop * PACK].rearrange("p (n i t) -> p n t i", i=RUN, t=PACK),
                in_=w_raw[pair, c][:, :, cols].rearrange("p t (n i) -> p n t i", i=RUN),
            )

        def quantize_w(pair, c):
            w_codes[pair, c] = keep.tile([P, PAIR_W], U32, name="w_codes%d_%d" % (pair, c), align_bytes=64)
            w_scales[pair, c] = keep.tile([P, PAIR_W], U8, name="w_scales%d_%d" % (pair, c), align_bytes=64)
            nc.vector.quantize_mx(out=w_codes[pair, c][:].bitcast(E4M3X4), scales=w_scales[pair, c][:], in_=w_grouped[pair, c][:])

        by_head = [(h, c) for h in range(2) for c in range(PASSES)]
        by_pass = [(h, c) for c in range(PASSES) for h in range(2)]

        def project(pair, half, steps):
            for h in range(2):
                sums[pair, half, h] = psum.tile([P, HALF_TOK], F32, name="sums", tag="mx%d" % half)
            for h, c in steps:
                cols = slice(h * DH, (h + 1) * DH)
                nc.tensor.matmul_mx(
                    out=sums[pair, half, h][:],
                    lhsT=w_codes[pair, c][:, cols].bitcast(E4M3X4),
                    lhsT_scale=w_scales[pair, c][:, cols],
                    rhs=x_codes[half, c][:].bitcast(E5M2X4),
                    rhs_scale=x_scales[half, c][:],
                    start=(c == 0),
                    stop=(c == PASSES - 1),
                )

        def bias_col(pair, h):
            return bias_cols[:, 2 * pair + h : 2 * pair + h + 1]

        def first_of(pair, half):
            return pair - 1 if pair - 1 in JOINED[half] else pair

        def result_cols(pair, half, name):
            first = first_of(pair, half)
            if pair == first:
                results[first, half] = work.tile([P, TILES, (2 if pair in JOINED[half] else 1) * PAIR_W], F32, name=name)
            return results[first, half][:, :, (pair - first) * PAIR_W : (pair - first + 1) * PAIR_W]

        def store(pair, half):
            if pair not in JOINED[half]:
                first = first_of(pair, half)
                dst = {K_PAIR: out_1, V_PAIR: out_2}.get(first, out_0)
                col0 = 0 if first in (K_PAIR, V_PAIR) else (first - 1) * PAIR_W
                src = results[first, half]
                rows = dst[0].rearrange("(half p t) h d -> p half t (h d)", p=P, t=TILES)
                nc.sync.dma_start(out=rows[:, half, :, col0 : col0 + src.shape[2]], in_=src[:])

        def copy_out(pair, half):
            result = result_cols(pair, half, "result_copied")
            for h in range(2):
                nc.scalar.copy(out=result[:, :, h * DH : (h + 1) * DH], in_=turned[pair, half, h][:])

        def negate_low_sin(half):
            low = sin_tok[half][:, :, LOW]
            nc.vector.tensor_scalar(out=low, in0=low, scalar1=-1.0, scalar2=None, op0=MULT)

        def turn_table(which, table, tag):
            bank = psum.tile([P, TILES, P], BF16, name="table_bank", tag=tag)
            for t in range(TILES):
                nc.tensor.transpose(bank[:, t, :], table[:, t, :], ident_bf[:])
            tables_chan[which] = keep.tile([P, HALF_TOK], BF16, name="table_chan%d" % which)
            nc.scalar.copy(out=tables_chan[which][:], in_=bank[:].rearrange("p t r -> p (t r)"))

        def multiply_chan(pair):
            for h in range(2):
                for which in range(2):
                    product = work.tile([P, HALF_TOK], F32, name="part_chan%d" % which)
                    chan_products[pair, h, which] = product
                    nc.vector.scalar_tensor_tensor(
                        out=product[:], in0=sums[pair, 0, h][:], scalar=bias_col(pair, h), in1=tables_chan[which][:], op0=ADD, op1=MULT
                    )

        def turn_and_add(pair):
            for h in range(2):
                turned[pair, 0, h] = psum.tile([P, TILES, DH], F32, name="turned", tag="tr0")
                for t in range(TILES):
                    for which, moving in enumerate((ident, swap)):
                        nc.tensor.matmul(
                            turned[pair, 0, h][:, t, :],
                            lhsT=chan_products[pair, h, which][:, t * P : (t + 1) * P],
                            rhs=moving[:],
                            is_transpose=True,
                            start=(which == 0),
                            stop=(which == 1),
                        )

        def add_bias(pair, half):
            for h in range(2):
                biased[pair, half, h] = work.tile([P, HALF_TOK], F32, name="biased", bufs=6)
                nc.scalar.activation(out=biased[pair, half, h][:], in_=sums[pair, half, h][:], func=IDENTITY, bias=bias_col(pair, h))

        def turn(pair, half, tag):
            for h in range(2):
                turned[pair, half, h] = psum.tile([P, TILES, DH], F32, name="turned", tag=tag)
                for t in range(TILES):
                    nc.tensor.transpose(turned[pair, half, h][:, t, :], biased[pair, half, h][:, t * P : (t + 1) * P], ident[:])

        def multiply_tok(pair, half, h):
            u = turned[pair, half, h]
            cos_u = work.tile([P, TILES, DH], F32, name="cos_u")
            sin_u = work.tile([P, TILES, DH], F32, name="sin_u")
            nc.vector.tensor_tensor(out=cos_u[:], in0=u[:], in1=cos_tok[half][:], op=MULT)
            nc.vector.tensor_tensor(out=sin_u[:, :, LOW], in0=u[:, :, HIGH], in1=sin_tok[half][:, :, LOW], op=MULT)
            nc.vector.tensor_tensor(out=sin_u[:, :, HIGH], in0=u[:, :, LOW], in1=sin_tok[half][:, :, HIGH], op=MULT)
            tok_products[pair, half, h] = (cos_u, sin_u)

        def add_tok(pair, half, h, engine):
            cos_u, sin_u = tok_products[pair, half, h]
            if h == 0:
                added[pair, half] = result_cols(pair, half, "result_added")
            engine.tensor_tensor(out=added[pair, half][:, :, h * DH : (h + 1) * DH], in0=cos_u[:], in1=sin_u[:], op=ADD)

        def rotate_tok(pair, half):
            for h in range(2):
                multiply_tok(pair, half, h)
                add_tok(pair, half, h, nc.gpsimd)

        on_scalar, on_vector = nc.scalar.copy, nc.vector.tensor_copy

        tags = ("mx0", "mx1", "tr0", "tr1")
        for duo in range(DUOS):
            for c in range(PASSES):
                transpose_x(duo, c, tags[(duo * PASSES + c) % len(tags)])
        for duo in range(2):
            for c, copy in enumerate((on_scalar, on_vector, on_scalar)):
                group_x(duo, c, copy)
            for c in range(PASSES):
                quantize_x(duo, c)
        for c in range(PASSES):
            group_x(2, c, on_scalar)
        group_x(3, 0, on_scalar)
        bias_bank = psum.tile([P, HEADS], F32, tag="mx1")
        nc.tensor.matmul(bias_bank[:], lhsT=bias_rows[:], rhs=ident_bf[:, 0:HEADS], start=True, stop=True)
        quantize_x(2, 0)
        quantize_x(2, 1)
        group_w(K_PAIR, 0, on_vector)
        quantize_x(2, 2)
        quantize_w(K_PAIR, 0)
        group_w(K_PAIR, 1, on_scalar)
        group_w(K_PAIR, 2, on_vector)
        quantize_w(K_PAIR, 1)
        quantize_w(K_PAIR, 2)
        bias_cols = keep.tile([P, HEADS], F32)
        nc.vector.tensor_copy(out=bias_cols[:], in_=bias_bank[:])

        project(K_PAIR, 0, by_pass)
        group_x(3, 1, on_scalar)
        group_x(3, 2, on_scalar)
        for c in range(PASSES):
            quantize_x(3, c)
        project(K_PAIR, 1, by_head)
        add_bias(K_PAIR, 0)
        negate_low_sin(0)
        sin_swapped = keep.tile([P, TILES, DH], BF16)
        nc.vector.tensor_copy(out=sin_swapped[:, :, LOW], in_=sin_tok[0][:, :, HIGH])
        nc.vector.tensor_copy(out=sin_swapped[:, :, HIGH], in_=sin_tok[0][:, :, LOW])
        turn(K_PAIR, 0, "tr0")
        add_bias(K_PAIR, 1)
        turn_table(0, cos_tok[0], "tr1")
        turn_table(1, sin_swapped, "tr1")

        group_w(V_PAIR, 0, on_vector)
        group_w(V_PAIR, 1, on_vector)
        quantize_w(V_PAIR, 0)
        group_w(V_PAIR, 2, on_vector)
        quantize_w(V_PAIR, 1)
        quantize_w(V_PAIR, 2)
        project(V_PAIR, 0, by_pass)
        multiply_tok(K_PAIR, 0, 0)
        add_tok(K_PAIR, 0, 0, nc.gpsimd)
        multiply_tok(K_PAIR, 0, 1)
        group_w(1, 0, on_scalar)
        add_bias(V_PAIR, 0)
        project(V_PAIR, 1, by_head)
        add_bias(V_PAIR, 1)
        group_w(1, 1, on_vector)
        quantize_w(1, 0)
        group_w(1, 2, on_vector)
        quantize_w(1, 1)
        quantize_w(1, 2)
        add_tok(K_PAIR, 0, 1, nc.vector)
        turn(V_PAIR, 0, "tr0")
        turn(V_PAIR, 1, "tr1")
        group_w(2, 0, on_scalar)
        copy_out(V_PAIR, 1)
        group_w(2, 1, on_scalar)
        store(K_PAIR, 0)
        store(V_PAIR, 1)

        for pair in range(1, LAST_Q):
            project(pair, 0, by_head)
            if pair > 1:
                copy_out(pair - 1, 0)
                store(pair - 1, 0)
                store(pair - 2, 1)
            if pair == LATE_LOAD_ROUND:
                load_two_query_pairs(LAST_Q - 1)
            multiply_chan(pair)
            project(pair, 1, by_head)
            if pair <= SHARED_ROUNDS:
                group_w(pair + 1, 2, on_scalar, slice(0, SCALAR_COLS))
                group_w(pair + 1, 2, on_vector, slice(SCALAR_COLS, PAIR_W))
            else:
                group_w(pair + 1, 2, on_scalar)
            for c in range(PASSES):
                quantize_w(pair + 1, c)
            if pair == 1:
                copy_out(V_PAIR, 0)
                store(V_PAIR, 0)
                negate_low_sin(1)
            add_bias(pair, 1)
            turn(pair - 1, 1, "tr1")
            rotate_tok(pair - 1, 1)
            turn_and_add(pair)
            if pair + 2 <= LAST_Q:
                group_w(pair + 2, 0, on_scalar)
                group_w(pair + 2, 1, on_scalar)

        project(LAST_Q, 0, by_head)
        copy_out(LAST_Q - 1, 0)
        store(LAST_Q - 1, 0)
        store(LAST_Q - 2, 1)
        multiply_chan(LAST_Q)
        turn(LAST_Q - 1, 1, "tr1")
        rotate_tok(LAST_Q - 1, 1)
        project(LAST_Q, 1, by_head)
        add_bias(LAST_Q, 1)
        turn_and_add(LAST_Q)
        turn(LAST_Q, 1, "mx0")
        copy_out(LAST_Q, 0)
        store(LAST_Q, 0)
        store(LAST_Q - 1, 1)
        multiply_tok(LAST_Q, 1, 0)
        add_tok(LAST_Q, 1, 0, nc.gpsimd)
        multiply_tok(LAST_Q, 1, 1)
        add_tok(LAST_Q, 1, 1, nc.vector)
        store(LAST_Q, 1)
